import numpy as np
import ml_dtypes


def mxq(x, axis, fmt="e4m3"):
    dtype, down = {"e4m3": (ml_dtypes.float8_e4m3fn, 7), "e5m2": (ml_dtypes.float8_e5m2, 14)}[fmt]
    v = np.moveaxis(np.asarray(x, np.float32).astype(ml_dtypes.bfloat16).astype(np.float64), axis, -1)
    blocks = v.reshape(v.shape[:-1] + (-1, 32))
    amax = np.abs(blocks).max(-1, keepdims=True)
    byte = np.maximum(np.where(amax > 0, np.frexp(amax)[1] - 1 + 127, 0) - down, 1)
    scale = np.exp2(byte - 127.0)
    codes = (blocks / scale).astype(np.float32).astype(dtype).astype(np.float64)
    return np.moveaxis((codes * scale).reshape(v.shape), -1, axis)


WIDE = False


def mx_kscale(k):
    if not WIDE:
        return np.ones(k)
    levels = np.array([10, -10, 5, -5, 0])
    a = np.random.permutation(np.resize(levels, k // 512 * 4)).reshape(k // 512, 4)
    idx = np.arange(k)
    return np.exp2(a[idx // 512, idx % 128 // 32])


BF16 = ml_dtypes.bfloat16


def bf(x):
    return np.asarray(x, np.float32).astype(BF16)


def f64(x):
    return np.asarray(x).astype(np.float64)


B, N, C, H, D, S = 4, 1024, 1024, 8, 128, 128
E = H * D


def setup_inputs():
    s = mx_kscale(C)
    return {"x": bf(np.random.standard_normal((B, N, C)) * s),
            "x_mid": bf(np.random.standard_normal((B, N, H, D))),
            "Wfx": bf(np.random.standard_normal((C, E)) / np.sqrt(C) / s[:, None]),
            "bfx": bf(np.random.standard_normal(E) * 0.2),
            "Wslice": bf(np.random.standard_normal((D, S)) * 2.0 / np.sqrt(D)),
            "bslice": bf(np.random.standard_normal(S) * 2.0),
            "temp": bf(np.random.uniform(0.5, 1.5, (1, 1, H, 1)))}


def reference(x, x_mid, Wfx, bfx, Wslice, bslice, temp):
    fx = (mxq(f64(x), 2, "e4m3") @ mxq(f64(Wfx), 0, "e4m3")) + f64(bfx)
    proj = f64(x_mid) @ f64(Wslice) + f64(bslice)
    z = proj / f64(temp)
    e = np.exp(z - z.max(-1, keepdims=True))
    slice_weights = e / e.sum(-1, keepdims=True)
    slice_norm = slice_weights.sum(1) + 0.01
    normed = slice_weights / slice_norm[:, None, :, :]
    a = normed.transpose(0, 2, 3, 1)
    f = fx.reshape(B, N, H, D).transpose(0, 2, 1, 3)
    return mxq(a, 3, "e4m3") @ mxq(f, 2, "e4m3")

@@ -1,0 +1,435 @@
+from contextlib import ExitStack
+
+import concourse.mybir as mybir
+from concourse.masks import make_identity
+
+F32 = mybir.dt.float32
+BF16 = mybir.dt.bfloat16
+U32 = mybir.dt.uint32
+U8 = mybir.dt.uint8
+FP8X4 = mybir.dt.float8_e4m3fn_x4
+ALU = mybir.AluOpType
+ACT = mybir.ActivationFunctionType
+AXIS_X = mybir.AxisListType.X
+
+B, N, C, H, D, S = 4, 1024, 1024, 8, 128, 128
+E = H * D
+P = 128
+PACK = 4
+K_PASS = P * PACK
+C_PASSES = C // K_PASS
+BLOCKS = N // K_PASS
+
+UNITS_PER_BATCH = H * BLOCKS
+UNITS = B * UNITS_PER_BATCH
+SLOTS_PER_BLOCK = PACK * C_PASSES
+SLOTS_PER_BATCH = BLOCKS * SLOTS_PER_BLOCK
+SLOTS = B * SLOTS_PER_BATCH
+
+X_TRANSPOSE = 0
+X_COPY = X_TRANSPOSE + 1
+X_QUANTISE = X_COPY + 1
+FX_MULTIPLY = SLOTS_PER_BATCH + X_QUANTISE + 2
+W_PIECES = 8
+W_REGROUP = FX_MULTIPLY - W_PIECES - 1
+W_QUANTISE = W_REGROUP + 1
+FX_BIAS = FX_MULTIPLY + 1
+FX_QUANTISE = FX_BIAS + 1
+XM_TRANSPOSE = 9
+XM_COPY = XM_TRANSPOSE + 1
+PROJECT = XM_COPY + 1
+LOGITS = PROJECT + 1
+EXP = LOGITS + 1
+INV_SUM = EXP + 1
+SCALE = INV_SUM + 1
+MASS = SCALE + 1
+INV_MASS = MASS + 1
+SPREAD = INV_MASS + 1
+SPREAD_COPY = SPREAD + 1
+NORMALISE = SPREAD_COPY + BLOCKS
+N_QUANTISE = NORMALISE + 1
+POOL = N_QUANTISE + 1
+OUT_COPY = POOL + 1
+STEPS = UNITS + OUT_COPY
+
+FLOPS = 2 * (B * N * C * E + B * N * H * D * S + B * H * S * D * N)
+
+
+def tile_physicsattentionbase_pa_t_kernel(tc, x, x_mid, Wfx, bfx, Wslice, bslice, temp, out):
+    nc = tc.nc
+    with ExitStack() as stack:
+        const = stack.enter_context(tc.tile_pool(name="const", bufs=1))
+        rows = stack.enter_context(tc.tile_pool(name="rows", bufs=2))
+        work = stack.enter_context(tc.tile_pool(name="work", bufs=2))
+        stats = stack.enter_context(tc.tile_pool(name="stats", bufs=3))
+        ps_tr = stack.enter_context(tc.psum_pool(name="ps_tr", bufs=2))
+        ps_proj = stack.enter_context(tc.psum_pool(name="ps_proj", bufs=2))
+        ps_fx = stack.enter_context(tc.psum_pool(name="ps_fx", bufs=2))
+        ps_mass = stack.enter_context(tc.psum_pool(name="ps_mass", bufs=1))
+        ps_misc = stack.enter_context(tc.psum_pool(name="ps_misc", bufs=1))
+        stack.enter_context(tc.manual_schedule())
+
+        x_rows = {}
+        xm_rows = {}
+        transposed = {}
+        x_grouped = {}
+        x_codes = {}
+        x_scales = {}
+        xm_t = {}
+        proj_ps = {}
+        w = {}
+        neg_max = {}
+        sum_exp = {}
+        inv_sum = {}
+        inv_mass = {}
+        spread_ps = {}
+        inv_mass_bc = {}
+        n_grouped = {}
+        n_codes = {}
+        n_scales = {}
+        fx_ps = {}
+        fx_grouped = {}
+        fx_codes = {}
+        fx_scales = {}
+        out_ps = {}
+
+        def unit(u):
+            b, rest = divmod(u, UNITS_PER_BATCH)
+            h, g = divmod(rest, BLOCKS)
+            return b, h, g
+
+        def is_unit(u):
+            return 0 <= u < UNITS
+
+        def ends_head(u):
+            return is_unit(u) and u % BLOCKS == BLOCKS - 1
+
+        def load_x(b, g):
+            x_rows[b, g] = rows.tile([P, PACK, C], BF16, name="x_rows", tag="x_rows", bufs=3)
+            nc.sync.dma_start(
+                out=x_rows[b, g][:].rearrange("p t c -> p (t c)"),
+                in_=x[b, g * K_PASS : (g + 1) * K_PASS, :].rearrange("(p t) c -> p (t c)", t=PACK),
+            )
+
+        def load_x_mid(b, g):
+            xm_rows[b, g] = rows.tile([P, PACK, E], BF16, name="xm_rows", tag="xm_rows", bufs=4)
+            nc.sync.dma_start(
+                out=xm_rows[b, g][:].rearrange("p t e -> p (t e)"),
+                in_=x_mid[b, g * K_PASS : (g + 1) * K_PASS].rearrange("(p t) h d -> p (t h d)", t=PACK),
+            )
+
+        def load_rows(step):
+            if step % SLOTS_PER_BLOCK == 0:
+                b, g = divmod(step // SLOTS_PER_BLOCK + 2, BLOCKS)
+                if b < B:
+                    load_x(b, g)
+            if step >= XM_TRANSPOSE and (step - XM_TRANSPOSE) % UNITS_PER_BATCH == 0:
+                b = (step - XM_TRANSPOSE) // UNITS_PER_BATCH + 1
+                if b < B:
+                    for g in range(BLOCKS):
+                        load_x_mid(b, g)
+
+        temp_bc = const.tile([P, H], BF16)
+        nc.scalar.dma_start(out=temp_bc[:], in_=temp.rearrange("a b h c -> (a b h c)").partition_broadcast(P))
+        bslice_bc = const.tile([P, S], BF16)
+        nc.scalar.dma_start(out=bslice_bc[:], in_=bslice.partition_broadcast(P))
+        wslice_sb = const.tile([P, S], BF16)
+        nc.scalar.dma_start(out=wslice_sb[:], in_=Wslice)
+        bfx_bc = const.tile([P, E], BF16)
+        nc.scalar.dma_start(out=bfx_bc[:], in_=bfx.partition_broadcast(P))
+
+        load_x(0, 0)
+        load_x_mid(0, 0)
+        load_x_mid(0, 1)
+        w_rows = []
+        for k in range(C_PASSES):
+            w_rows_k = rows.tile([P, PACK, E], BF16, tag="w_rows")
+            nc.sync.dma_start(
+                out=w_rows_k[:].rearrange("q (u e) c -> q u (e c)", u=2),
+                in_=Wfx[k * K_PASS : (k + 1) * K_PASS, :].rearrange("(u q e) c -> q u (e c)", u=2, e=2),
+            )
+            w_rows.append(w_rows_k)
+        load_x(0, 1)
+
+        ident_f32 = const.tile([P, P], F32)
+        make_identity(nc, ident_f32[:])
+        ident_bf = const.tile([P, P], BF16)
+        make_identity(nc, ident_bf[:])
+        ones_col = const.tile([P, 1], F32)
+        nc.vector.memset(ones_col[:], 1.0)
+
+        temp_f32 = const.tile([P, H], F32)
+        nc.vector.tensor_copy(out=temp_f32[:], in_=temp_bc[:])
+        inv_temp = const.tile([P, H], F32)
+        nc.vector.reciprocal(out=inv_temp[:], in_=temp_f32[:])
+        bias_over_temp = const.tile([P, H, S], F32)
+        for h in range(H):
+            nc.vector.tensor_scalar_mul(out=bias_over_temp[:, h, :], in0=bslice_bc[:], scalar1=inv_temp[:, h : h + 1])
+
+        w_codes = const.tile([P, C_PASSES, E], U32, align_bytes=64)
+        w_scales = const.tile([P, C_PASSES, E], U8, align_bytes=64)
+        w_grouped = {}
+        W_COLS = C_PASSES * E // W_PIECES
+
+        def regroup_w(piece):
+            if not 0 <= piece < W_PIECES:
+                return
+            k, part = divmod(piece, W_PIECES // C_PASSES)
+            w_grouped[piece] = work.tile([P, W_COLS, PACK], BF16, name="w_grouped", tag="w_grouped", align_bytes=64)
+            nc.vector.tensor_copy(
+                out=w_grouped[piece][:],
+                in_=w_rows[k][:, :, part * W_COLS : (part + 1) * W_COLS].rearrange("q j c -> q c j"),
+            )
+
+        def quantise_w(piece):
+            if not 0 <= piece < W_PIECES:
+                return
+            k, part = divmod(piece, W_PIECES // C_PASSES)
+            nc.vector.quantize_mx(
+                out=w_codes[:, k, part * W_COLS : (part + 1) * W_COLS].bitcast(FP8X4),
+                scales=w_scales[:, k, part * W_COLS : (part + 1) * W_COLS],
+                in_=w_grouped[piece][:].rearrange("q c j -> q (c j)"),
+            )
+
+        mass_ps = ps_mass.tile([P, B * H], F32)
+
+        def transpose_rows(step):
+            u = step - XM_TRANSPOSE
+            i = step - X_TRANSPOSE
+            if not (is_unit(u) or 0 <= i < SLOTS):
+                return
+            bank = ps_tr.tile([P, 2 * PACK * P], BF16, name="transposed", tag="transposed")
+            transposed[step] = bank
+            if is_unit(u):
+                b, h, g = unit(u)
+                for t in range(PACK):
+                    nc.tensor.transpose(bank[:, t * P : (t + 1) * P], xm_rows[b, g][:, t, h * D : (h + 1) * D], ident_bf[:])
+            if 0 <= i < SLOTS:
+                block, rest = divmod(i, SLOTS_PER_BLOCK)
+                b, g = divmod(block, BLOCKS)
+                t, k = divmod(rest, C_PASSES)
+                words = x_rows[b, g][:, t, :].bitcast(F32)
+                pairs = bank[:, PACK * P :].bitcast(F32)
+                for half in range(2):
+                    first = (k * 2 + half) * P
+                    nc.tensor.transpose(pairs[:, half * P : (half + 1) * P], words[:, first : first + P], ident_f32[:])
+
+        def copy_transposed(step):
+            u = step - XM_COPY
+            if is_unit(u):
+                xm_t[u] = work.tile([P, PACK, P], BF16, name="xm_t", tag="xm_t", bufs=3)
+                bank = transposed[u + XM_TRANSPOSE]
+                nc.scalar.copy(out=xm_t[u][:].rearrange("d t p -> d (t p)"), in_=bank[:, : PACK * P])
+            i = step - X_COPY
+            if 0 <= i < SLOTS:
+                x_grouped[i] = work.tile([P, P, PACK], BF16, name="x_grouped", tag="x_grouped", bufs=3, align_bytes=64)
+                pairs = transposed[i + X_TRANSPOSE][:, PACK * P :].bitcast(F32)
+                nc.scalar.copy(
+                    out=x_grouped[i][:].bitcast(F32),
+                    in_=pairs.rearrange("q (u p) -> q p u", u=2),
+                )
+
+        def quantise_x(i):
+            if not 0 <= i < SLOTS:
+                return
+            b, slot = divmod(i, SLOTS_PER_BATCH)
+            if slot == 0:
+                x_codes[b] = work.tile([P, SLOTS_PER_BATCH, P], U32, name="x_codes", tag="x_codes", bufs=3, align_bytes=64)
+                x_scales[b] = work.tile([P, SLOTS_PER_BATCH, P], U8, name="x_scales", tag="x_scales", bufs=3, align_bytes=64)
+            nc.vector.quantize_mx(
+                out=x_codes[b][:, slot, :].bitcast(FP8X4),
+                scales=x_scales[b][:, slot, :],
+                in_=x_grouped[i][:].rearrange("q p j -> q (p j)"),
+            )
+
+        def project(u):
+            if not is_unit(u):
+                return
+            proj_ps[u] = ps_proj.tile([P, PACK, S], F32, name="proj_ps", tag="proj_ps")
+            for t in range(PACK):
+                nc.tensor.matmul(out=proj_ps[u][:, t, :], lhsT=xm_t[u][:, t, :], rhs=wslice_sb[:], start=True, stop=True)
+
+        def logits(u):
+            if not is_unit(u):
+                return
+            b, h, g = unit(u)
+            w[u] = work.tile([P, PACK, S], F32, name="w", tag="w", bufs=12)
+            nc.vector.scalar_tensor_tensor(
+                out=w[u][:],
+                in0=proj_ps[u][:],
+                scalar=inv_temp[:, h : h + 1],
+                in1=bias_over_temp[:, h, :].unsqueeze(1).to_broadcast([P, PACK, S]),
+                op0=ALU.mult,
+                op1=ALU.add,
+            )
+
+        def row_max(u):
+            if not is_unit(u):
+                return
+            neg_max[u] = stats.tile([P, PACK], F32, name="neg_max", tag="neg_max")
+            nc.vector.tensor_reduce(out=neg_max[u][:], in_=w[u][:], axis=AXIS_X, op=ALU.max, negate=True)
+
+        def exponentials(u):
+            if not is_unit(u):
+                return
+            sum_exp[u] = stats.tile([P, PACK], F32, name="sum_exp", tag="sum_exp")
+            for t in range(PACK):
+                nc.scalar.activation(
+                    out=w[u][:, t, :],
+                    in_=w[u][:, t, :],
+                    func=ACT.Exp,
+                    bias=neg_max[u][:, t : t + 1],
+                    scale=1.0,
+                    accum_out=sum_exp[u][:, t : t + 1],
+                )
+
+        def invert_sums(u):
+            if not is_unit(u):
+                return
+            inv_sum[u] = stats.tile([P, PACK], F32, name="inv_sum", tag="inv_sum")
+            nc.vector.reciprocal(out=inv_sum[u][:], in_=sum_exp[u][:])
+
+        def scale_rows(u):
+            if not is_unit(u):
+                return
+            for t in range(PACK):
+                nc.scalar.activation(out=w[u][:, t, :], in_=w[u][:, t, :], func=ACT.Copy, scale=inv_sum[u][:, t : t + 1])
+
+        def add_mass(u):
+            if not is_unit(u):
+                return
+            b, h, g = unit(u)
+            for t in range(PACK):
+                nc.tensor.matmul(
+                    out=mass_ps[:, b * H + h : b * H + h + 1],
+                    lhsT=w[u][:, t, :],
+                    rhs=ones_col[:],
+                    start=(g == 0 and t == 0),
+                    stop=(g == BLOCKS - 1 and t == PACK - 1),
+                )
+
+        def invert_mass(u):
+            if not ends_head(u):
+                return
+            b, h, g = unit(u)
+            mass_eps = stats.tile([P, 1], F32, tag="mass_eps")
+            nc.vector.tensor_scalar_add(out=mass_eps[:], in0=mass_ps[:, b * H + h : b * H + h + 1], scalar1=0.01)
+            inv_mass[u] = stats.tile([P, 1], F32, name="inv_mass", tag="inv_mass")
+            nc.vector.reciprocal(out=inv_mass[u][:], in_=mass_eps[:])
+
+        def spread_inv_mass(u):
+            if not ends_head(u):
+                return
+            spread_ps[u] = ps_misc.tile([P, S], F32, name="spread_ps", tag="misc")
+            nc.tensor.matmul(out=spread_ps[u][:], lhsT=inv_mass[u][:].to_broadcast([P, P]), rhs=ident_f32[:], start=True, stop=True)
+
+        def copy_spread(u):
+            if not ends_head(u):
+                return
+            inv_mass_bc[u] = stats.tile([P, S], F32, name="inv_mass_bc", tag="inv_mass_bc")
+            nc.scalar.copy(out=inv_mass_bc[u][:], in_=spread_ps[u][:])
+
+        def normalise(u):
+            if not is_unit(u):
+                return
+            n_grouped[u] = work.tile([P, S, PACK], BF16, name="n_grouped", tag="n_grouped", bufs=3, align_bytes=64)
+            head_end = u - u % BLOCKS + BLOCKS - 1
+            nc.gpsimd.tensor_tensor(
+                out=n_grouped[u][:],
+                in0=w[u][:].rearrange("p t s -> p s t"),
+                in1=inv_mass_bc[head_end][:].unsqueeze(2).to_broadcast([P, S, PACK]),
+                op=ALU.mult,
+            )
+
+        def quantise_unit(u, grouped, codes, scales, name):
+            if not is_unit(u):
+                return
+            b, i = divmod(u, UNITS_PER_BATCH)
+            if i == 0:
+                codes[b] = work.tile([P, UNITS_PER_BATCH, P], U32, name=name + "_codes", tag=name + "_codes", align_bytes=64)
+                scales[b] = work.tile([P, UNITS_PER_BATCH, P], U8, name=name + "_scales", tag=name + "_scales", align_bytes=64)
+            nc.vector.quantize_mx(
+                out=codes[b][:, i, :].bitcast(FP8X4),
+                scales=scales[b][:, i, :],
+                in_=grouped[u][:].rearrange("p c t -> p (c t)"),
+            )
+
+        def multiply_features(u):
+            if not is_unit(u):
+                return
+            b, h, g = unit(u)
+            fx_ps[u] = ps_fx.tile([P, PACK, D], F32, name="fx_ps", tag="fx_ps")
+            for t in range(PACK):
+                for k in range(C_PASSES):
+                    i = (g * PACK + t) * C_PASSES + k
+                    nc.tensor.matmul_mx(
+                        out=fx_ps[u][:, t, :],
+                        lhsT=x_codes[b][:, i, :].bitcast(FP8X4),
+                        lhsT_scale=x_scales[b][:, i, :],
+                        rhs=w_codes[:, k, h * D : (h + 1) * D].bitcast(FP8X4),
+                        rhs_scale=w_scales[:, k, h * D : (h + 1) * D],
+                        start=(k == 0),
+                        stop=(k == C_PASSES - 1),
+                    )
+
+        def add_feature_bias(u):
+            if not is_unit(u):
+                return
+            b, h, g = unit(u)
+            fx_grouped[u] = work.tile([P, D, PACK], BF16, name="fx_grouped", tag="fx_grouped", bufs=3, align_bytes=64)
+            nc.vector.tensor_tensor(
+                out=fx_grouped[u][:],
+                in0=fx_ps[u][:].rearrange("p t d -> p d t"),
+                in1=bfx_bc[:, h * D : (h + 1) * D].unsqueeze(2).to_broadcast([P, D, PACK]),
+                op=ALU.add,
+            )
+
+        def pool_points(u):
+            if not ends_head(u):
+                return
+            b, h, g = unit(u)
+            out_ps[u] = ps_misc.tile([P, D], F32, name="out_ps", tag="misc")
+            for g in range(BLOCKS):
+                i = h * BLOCKS + g
+                nc.tensor.matmul_mx(
+                    out=out_ps[u][:],
+                    lhsT=n_codes[b][:, i, :].bitcast(FP8X4),
+                    lhsT_scale=n_scales[b][:, i, :],
+                    rhs=fx_codes[b][:, i, :].bitcast(FP8X4),
+                    rhs_scale=fx_scales[b][:, i, :],
+                    start=(g == 0),
+                    stop=(g == BLOCKS - 1),
+                )
+
+        def copy_out(u):
+            if not ends_head(u):
+                return
+            b, h, g = unit(u)
+            out_sb = work.tile([P, D], F32, tag="out_sb", bufs=4)
+            nc.scalar.copy(out=out_sb[:], in_=out_ps[u][:])
+            nc.scalar.dma_start(out=out[b, h], in_=out_sb[:])
+
+        for step in range(STEPS):
+            load_rows(step)
+            copy_spread(step - SPREAD_COPY)
+            copy_out(step - OUT_COPY)
+            copy_transposed(step)
+            project(step - PROJECT)
+            add_mass(step - MASS)
+            spread_inv_mass(step - SPREAD)
+            logits(step - LOGITS)
+            multiply_features(step - FX_MULTIPLY)
+            pool_points(step - POOL)
+            add_feature_bias(step - FX_BIAS)
+            row_max(step - LOGITS)
+            exponentials(step - EXP)
+            invert_sums(step - INV_SUM)
+            scale_rows(step - SCALE)
+            invert_mass(step - INV_MASS)
+            transpose_rows(step)
+            normalise(step - NORMALISE)
+            quantise_x(step - X_QUANTISE)
+            quantise_unit(step - FX_QUANTISE, fx_grouped, fx_codes, fx_scales, "fx")
+            quantise_unit(step - N_QUANTISE, n_grouped, n_codes, n_scales, "n")
+            quantise_w(step - W_QUANTISE)
+            regroup_w(step - W_REGROUP)

@@ -35,7 +35,7 @@ W_REGROUP = FX_MULTIPLY - W_PIECES - 1
 W_QUANTISE = W_REGROUP + 1
 FX_BIAS = FX_MULTIPLY + 1
 FX_QUANTISE = FX_BIAS + 1
-XM_TRANSPOSE = 9
+XM_TRANSPOSE = 8
 XM_COPY = XM_TRANSPOSE + 1
 PROJECT = XM_COPY + 1
 LOGITS = PROJECT + 1
@@ -43,7 +43,8 @@ EXP = LOGITS + 1
 INV_SUM = EXP + 1
 SCALE = INV_SUM + 1
 MASS = SCALE + 1
-INV_MASS = MASS + 1
+SUM_MASS = MASS + 1
+INV_MASS = SUM_MASS + 1
 SPREAD = INV_MASS + 1
 SPREAD_COPY = SPREAD + 1
 NORMALISE = SPREAD_COPY + BLOCKS
@@ -81,6 +82,7 @@ def tile_physicsattentionbase_pa_t_kernel(tc, x, x_mid, Wfx, bfx, Wslice, bslice
         neg_max = {}
         sum_exp = {}
         inv_sum = {}
+        mass = {}
         inv_mass = {}
         spread_ps = {}
         inv_mass_bc = {}
@@ -155,8 +157,6 @@ def tile_physicsattentionbase_pa_t_kernel(tc, x, x_mid, Wfx, bfx, Wslice, bslice
         make_identity(nc, ident_f32[:])
         ident_bf = const.tile([P, P], BF16)
         make_identity(nc, ident_bf[:])
-        ones_col = const.tile([P, 1], F32)
-        nc.vector.memset(ones_col[:], 1.0)
 
         temp_f32 = const.tile([P, H], F32)
         nc.vector.tensor_copy(out=temp_f32[:], in_=temp_bc[:])
@@ -191,7 +191,8 @@ def tile_physicsattentionbase_pa_t_kernel(tc, x, x_mid, Wfx, bfx, Wslice, bslice
                 in_=w_grouped[piece][:].rearrange("q c j -> q (c j)"),
             )
 
-        mass_ps = ps_mass.tile([P, B * H], F32)
+        MASS_REGIONS = 4
+        mass_ps = ps_mass.tile([P, MASS_REGIONS, P], F32)
 
         def transpose_rows(step):
             u = step - XM_TRANSPOSE
@@ -253,7 +254,7 @@ def tile_physicsattentionbase_pa_t_kernel(tc, x, x_mid, Wfx, bfx, Wslice, bslice
             if not is_unit(u):
                 return
             b, h, g = unit(u)
-            w[u] = work.tile([P, PACK, S], F32, name="w", tag="w", bufs=12)
+            w[u] = work.tile([P, PACK, S], F32, name="w", tag="w", bufs=13)
             nc.vector.scalar_tensor_tensor(
                 out=w[u][:],
                 in0=proj_ps[u][:],
@@ -301,19 +302,27 @@ def tile_physicsattentionbase_pa_t_kernel(tc, x, x_mid, Wfx, bfx, Wslice, bslice
             b, h, g = unit(u)
             for t in range(PACK):
                 nc.tensor.matmul(
-                    out=mass_ps[:, b * H + h : b * H + h + 1],
+                    out=mass_ps[:, h % MASS_REGIONS, :],
                     lhsT=w[u][:, t, :],
-                    rhs=ones_col[:],
+                    rhs=ident_f32[:],
+                    is_transpose=True,
                     start=(g == 0 and t == 0),
                     stop=(g == BLOCKS - 1 and t == PACK - 1),
                 )
 
-        def invert_mass(u):
+        def sum_mass(u):
             if not ends_head(u):
                 return
             b, h, g = unit(u)
+            mass[u] = stats.tile([P, 1], F32, name="mass", tag="mass")
+            unread = stats.tile([P, P], F32, tag="unread")
+            nc.scalar.activation(out=unread[:], in_=mass_ps[:, h % MASS_REGIONS, :], func=ACT.Copy, accum_out=mass[u][:])
+
+        def invert_mass(u):
+            if not ends_head(u):
+                return
             mass_eps = stats.tile([P, 1], F32, tag="mass_eps")
-            nc.vector.tensor_scalar_add(out=mass_eps[:], in0=mass_ps[:, b * H + h : b * H + h + 1], scalar1=0.01)
+            nc.vector.tensor_scalar_add(out=mass_eps[:], in0=mass[u][:], scalar1=0.01)
             inv_mass[u] = stats.tile([P, 1], F32, name="inv_mass", tag="inv_mass")
             nc.vector.reciprocal(out=inv_mass[u][:], in_=mass_eps[:])
 
@@ -321,7 +330,7 @@ def tile_physicsattentionbase_pa_t_kernel(tc, x, x_mid, Wfx, bfx, Wslice, bslice
             if not ends_head(u):
                 return
             spread_ps[u] = ps_misc.tile([P, S], F32, name="spread_ps", tag="misc")
-            nc.tensor.matmul(out=spread_ps[u][:], lhsT=inv_mass[u][:].to_broadcast([P, P]), rhs=ident_f32[:], start=True, stop=True)
+            nc.tensor.transpose(spread_ps[u][:], inv_mass[u][:].to_broadcast([P, P]), ident_f32[:])
 
         def copy_spread(u):
             if not ends_head(u):
@@ -413,10 +422,9 @@ def tile_physicsattentionbase_pa_t_kernel(tc, x, x_mid, Wfx, bfx, Wslice, bslice
             load_rows(step)
             copy_spread(step - SPREAD_COPY)
             copy_out(step - OUT_COPY)
+            sum_mass(step - SUM_MASS)
             copy_transposed(step)
             project(step - PROJECT)
-            add_mass(step - MASS)
-            spread_inv_mass(step - SPREAD)
             logits(step - LOGITS)
             multiply_features(step - FX_MULTIPLY)
             pool_points(step - POOL)
@@ -427,6 +435,8 @@ def tile_physicsattentionbase_pa_t_kernel(tc, x, x_mid, Wfx, bfx, Wslice, bslice
             scale_rows(step - SCALE)
             invert_mass(step - INV_MASS)
             transpose_rows(step)
+            add_mass(step - MASS)
+            spread_inv_mass(step - SPREAD)
             normalise(step - NORMALISE)
             quantise_x(step - X_QUANTISE)
             quantise_unit(step - FX_QUANTISE, fx_grouped, fx_codes, fx_scales, "fx")

@@ -341,7 +341,7 @@ def tile_physicsattentionbase_pa_t_kernel(tc, x, x_mid, Wfx, bfx, Wslice, bslice
         def normalise(u):
             if not is_unit(u):
                 return
-            n_grouped[u] = work.tile([P, S, PACK], BF16, name="n_grouped", tag="n_grouped", bufs=3, align_bytes=64)
+            n_grouped[u] = work.tile([P, S, PACK], BF16, name="n_grouped", tag="n_grouped", bufs=1, align_bytes=64)
             head_end = u - u % BLOCKS + BLOCKS - 1
             nc.gpsimd.tensor_tensor(
                 out=n_grouped[u][:],
@@ -437,9 +437,9 @@ def tile_physicsattentionbase_pa_t_kernel(tc, x, x_mid, Wfx, bfx, Wslice, bslice
             transpose_rows(step)
             add_mass(step - MASS)
             spread_inv_mass(step - SPREAD)
-            normalise(step - NORMALISE)
             quantise_x(step - X_QUANTISE)
             quantise_unit(step - FX_QUANTISE, fx_grouped, fx_codes, fx_scales, "fx")
             quantise_unit(step - N_QUANTISE, n_grouped, n_codes, n_scales, "n")
             quantise_w(step - W_QUANTISE)
             regroup_w(step - W_REGROUP)
+            normalise(step - NORMALISE)

@@ -39,15 +39,14 @@ XM_TRANSPOSE = 8
 XM_COPY = XM_TRANSPOSE + 1
 PROJECT = XM_COPY + 1
 LOGITS = PROJECT + 1
-EXP = LOGITS + 1
+ROW_MAX = LOGITS
+EXP = ROW_MAX + 2
 INV_SUM = EXP + 1
-SCALE = INV_SUM + 1
+SCALE = INV_SUM + 2
 MASS = SCALE + 1
-SUM_MASS = MASS + 1
-INV_MASS = SUM_MASS + 1
-SPREAD = INV_MASS + 1
-SPREAD_COPY = SPREAD + 1
-NORMALISE = SPREAD_COPY + BLOCKS
+INV_MASS = MASS + 1
+SPREAD_COPY = INV_MASS + 1
+NORMALISE = SPREAD_COPY + 2
 N_QUANTISE = NORMALISE + 1
 POOL = N_QUANTISE + 1
 OUT_COPY = POOL + 1
@@ -223,24 +222,25 @@ def tile_physicsattentionbase_pa_t_kernel(tc, x, x_mid, Wfx, bfx, Wslice, bslice
                 nc.scalar.copy(out=xm_t[u][:].rearrange("d t p -> d (t p)"), in_=bank[:, : PACK * P])
             i = step - X_COPY
             if 0 <= i < SLOTS:
-                x_grouped[i] = work.tile([P, P, PACK], BF16, name="x_grouped", tag="x_grouped", bufs=3, align_bytes=64)
+                if i % 2 == 0:
+                    x_grouped[i // 2] = work.tile([P, 2, P, PACK], BF16, name="x_grouped", tag="x_grouped", bufs=3, align_bytes=64)
                 pairs = transposed[i + X_TRANSPOSE][:, PACK * P :].bitcast(F32)
                 nc.scalar.copy(
-                    out=x_grouped[i][:].bitcast(F32),
+                    out=x_grouped[i // 2][:, i % 2].bitcast(F32),
                     in_=pairs.rearrange("q (u p) -> q p u", u=2),
                 )
 
         def quantise_x(i):
-            if not 0 <= i < SLOTS:
+            if not (0 <= i < SLOTS and i % 2 == 1):
                 return
             b, slot = divmod(i, SLOTS_PER_BATCH)
-            if slot == 0:
+            if slot == 1:
                 x_codes[b] = work.tile([P, SLOTS_PER_BATCH, P], U32, name="x_codes", tag="x_codes", bufs=3, align_bytes=64)
                 x_scales[b] = work.tile([P, SLOTS_PER_BATCH, P], U8, name="x_scales", tag="x_scales", bufs=3, align_bytes=64)
             nc.vector.quantize_mx(
-                out=x_codes[b][:, slot, :].bitcast(FP8X4),
-                scales=x_scales[b][:, slot, :],
-                in_=x_grouped[i][:].rearrange("q p j -> q (p j)"),
+                out=x_codes[b][:, slot - 1 : slot + 1].rearrange("q i p -> q (i p)").bitcast(FP8X4),
+                scales=x_scales[b][:, slot - 1 : slot + 1].rearrange("q i p -> q (i p)"),
+                in_=x_grouped[i // 2][:].rearrange("q i p j -> q (i p j)"),
             )
 
         def project(u):
@@ -254,9 +254,10 @@ def tile_physicsattentionbase_pa_t_kernel(tc, x, x_mid, Wfx, bfx, Wslice, bslice
             if not is_unit(u):
                 return
             b, h, g = unit(u)
-            w[u] = work.tile([P, PACK, S], F32, name="w", tag="w", bufs=13)
+            if g == 0:
+                w[u // BLOCKS] = work.tile([P, BLOCKS, PACK, S], F32, name="w", tag="w", bufs=8)
             nc.vector.scalar_tensor_tensor(
-                out=w[u][:],
+                out=w[u // BLOCKS][:, g],
                 in0=proj_ps[u][:],
                 scalar=inv_temp[:, h : h + 1],
                 in1=bias_over_temp[:, h, :].unsqueeze(1).to_broadcast([P, PACK, S]),
@@ -265,36 +266,43 @@ def tile_physicsattentionbase_pa_t_kernel(tc, x, x_mid, Wfx, bfx, Wslice, bslice
             )
 
         def row_max(u):
-            if not is_unit(u):
+            if not ends_head(u):
                 return
-            neg_max[u] = stats.tile([P, PACK], F32, name="neg_max", tag="neg_max")
-            nc.vector.tensor_reduce(out=neg_max[u][:], in_=w[u][:], axis=AXIS_X, op=ALU.max, negate=True)
+            head = u // BLOCKS
+            neg_max[head] = stats.tile([P, BLOCKS, PACK], F32, name="neg_max", tag="neg_max")
+            nc.vector.tensor_reduce(out=neg_max[head][:], in_=w[head][:], axis=AXIS_X, op=ALU.max, negate=True)
 
         def exponentials(u):
             if not is_unit(u):
                 return
-            sum_exp[u] = stats.tile([P, PACK], F32, name="sum_exp", tag="sum_exp")
+            head, g = divmod(u, BLOCKS)
+            if g == 0:
+                sum_exp[head] = stats.tile([P, BLOCKS, PACK], F32, name="sum_exp", tag="sum_exp")
             for t in range(PACK):
                 nc.scalar.activation(
-                    out=w[u][:, t, :],
-                    in_=w[u][:, t, :],
+                    out=w[head][:, g, t, :],
+                    in_=w[head][:, g, t, :],
                     func=ACT.Exp,
-                    bias=neg_max[u][:, t : t + 1],
+                    bias=neg_max[head][:, g, t : t + 1],
                     scale=1.0,
-                    accum_out=sum_exp[u][:, t : t + 1],
+                    accum_out=sum_exp[head][:, g, t : t + 1],
                 )
 
         def invert_sums(u):
-            if not is_unit(u):
+            if not ends_head(u):
                 return
-            inv_sum[u] = stats.tile([P, PACK], F32, name="inv_sum", tag="inv_sum")
-            nc.vector.reciprocal(out=inv_sum[u][:], in_=sum_exp[u][:])
+            head = u // BLOCKS
+            inv_sum[head] = stats.tile([P, BLOCKS, PACK], F32, name="inv_sum", tag="inv_sum")
+            nc.vector.reciprocal(out=inv_sum[head][:], in_=sum_exp[head][:])
 
         def scale_rows(u):
             if not is_unit(u):
                 return
+            head, g = divmod(u, BLOCKS)
             for t in range(PACK):
-                nc.scalar.activation(out=w[u][:, t, :], in_=w[u][:, t, :], func=ACT.Copy, scale=inv_sum[u][:, t : t + 1])
+                nc.scalar.activation(
+                    out=w[head][:, g, t, :], in_=w[head][:, g, t, :], func=ACT.Copy, scale=inv_sum[head][:, g, t : t + 1]
+                )
 
         def add_mass(u):
             if not is_unit(u):
@@ -303,7 +311,7 @@ def tile_physicsattentionbase_pa_t_kernel(tc, x, x_mid, Wfx, bfx, Wslice, bslice
             for t in range(PACK):
                 nc.tensor.matmul(
                     out=mass_ps[:, h % MASS_REGIONS, :],
-                    lhsT=w[u][:, t, :],
+                    lhsT=w[u // BLOCKS][:, g, t, :],
                     rhs=ident_f32[:],
                     is_transpose=True,
                     start=(g == 0 and t == 0),
@@ -341,26 +349,28 @@ def tile_physicsattentionbase_pa_t_kernel(tc, x, x_mid, Wfx, bfx, Wslice, bslice
         def normalise(u):
             if not is_unit(u):
                 return
-            n_grouped[u] = work.tile([P, S, PACK], BF16, name="n_grouped", tag="n_grouped", bufs=1, align_bytes=64)
-            head_end = u - u % BLOCKS + BLOCKS - 1
+            head, g = divmod(u, BLOCKS)
+            if g == 0:
+                n_grouped[head] = work.tile([P, BLOCKS, S, PACK], BF16, name="n_grouped", tag="n_grouped", bufs=3, align_bytes=64)
+            head_end = u - g + BLOCKS - 1
             nc.gpsimd.tensor_tensor(
-                out=n_grouped[u][:],
-                in0=w[u][:].rearrange("p t s -> p s t"),
+                out=n_grouped[head][:, g],
+                in0=w[head][:, g].rearrange("p t s -> p s t"),
                 in1=inv_mass_bc[head_end][:].unsqueeze(2).to_broadcast([P, S, PACK]),
                 op=ALU.mult,
             )
 
-        def quantise_unit(u, grouped, codes, scales, name):
-            if not is_unit(u):
+        def quantise_head(u, grouped, codes, scales, name):
+            if not ends_head(u):
                 return
             b, i = divmod(u, UNITS_PER_BATCH)
-            if i == 0:
+            if i == BLOCKS - 1:
                 codes[b] = work.tile([P, UNITS_PER_BATCH, P], U32, name=name + "_codes", tag=name + "_codes", align_bytes=64)
                 scales[b] = work.tile([P, UNITS_PER_BATCH, P], U8, name=name + "_scales", tag=name + "_scales", align_bytes=64)
             nc.vector.quantize_mx(
-                out=codes[b][:, i, :].bitcast(FP8X4),
-                scales=scales[b][:, i, :],
-                in_=grouped[u][:].rearrange("p c t -> p (c t)"),
+                out=codes[b][:, i - BLOCKS + 1 : i + 1].rearrange("p g c -> p (g c)").bitcast(FP8X4),
+                scales=scales[b][:, i - BLOCKS + 1 : i + 1].rearrange("p g c -> p (g c)"),
+                in_=grouped[u // BLOCKS][:].rearrange("p g c t -> p (g c t)"),
             )
 
         def multiply_features(u):
@@ -385,9 +395,10 @@ def tile_physicsattentionbase_pa_t_kernel(tc, x, x_mid, Wfx, bfx, Wslice, bslice
             if not is_unit(u):
                 return
             b, h, g = unit(u)
-            fx_grouped[u] = work.tile([P, D, PACK], BF16, name="fx_grouped", tag="fx_grouped", bufs=3, align_bytes=64)
+            if g == 0:
+                fx_grouped[u // BLOCKS] = work.tile([P, BLOCKS, D, PACK], BF16, name="fx_grouped", tag="fx_grouped", bufs=3, align_bytes=64)
             nc.vector.tensor_tensor(
-                out=fx_grouped[u][:],
+                out=fx_grouped[u // BLOCKS][:, g],
                 in0=fx_ps[u][:].rearrange("p t d -> p d t"),
                 in1=bfx_bc[:, h * D : (h + 1) * D].unsqueeze(2).to_broadcast([P, D, PACK]),
                 op=ALU.add,
@@ -422,24 +433,24 @@ def tile_physicsattentionbase_pa_t_kernel(tc, x, x_mid, Wfx, bfx, Wslice, bslice
             load_rows(step)
             copy_spread(step - SPREAD_COPY)
             copy_out(step - OUT_COPY)
-            sum_mass(step - SUM_MASS)
+            sum_mass(step - INV_MASS)
             copy_transposed(step)
             project(step - PROJECT)
             logits(step - LOGITS)
             multiply_features(step - FX_MULTIPLY)
             pool_points(step - POOL)
             add_feature_bias(step - FX_BIAS)
-            row_max(step - LOGITS)
+            invert_mass(step - INV_MASS)
+            row_max(step - ROW_MAX)
             exponentials(step - EXP)
             invert_sums(step - INV_SUM)
             scale_rows(step - SCALE)
-            invert_mass(step - INV_MASS)
             transpose_rows(step)
             add_mass(step - MASS)
-            spread_inv_mass(step - SPREAD)
+            spread_inv_mass(step - INV_MASS)
+            normalise(step - NORMALISE)
             quantise_x(step - X_QUANTISE)
-            quantise_unit(step - FX_QUANTISE, fx_grouped, fx_codes, fx_scales, "fx")
-            quantise_unit(step - N_QUANTISE, n_grouped, n_codes, n_scales, "n")
+            quantise_head(step - FX_QUANTISE, fx_grouped, fx_codes, fx_scales, "fx")
+            quantise_head(step - N_QUANTISE, n_grouped, n_codes, n_scales, "n")
             quantise_w(step - W_QUANTISE)
             regroup_w(step - W_REGROUP)
-            normalise(step - NORMALISE)

@@ -26,16 +26,7 @@ SLOTS_PER_BLOCK = PACK * C_PASSES
 SLOTS_PER_BATCH = BLOCKS * SLOTS_PER_BLOCK
 SLOTS = B * SLOTS_PER_BATCH
 
-X_TRANSPOSE = 0
-X_COPY = X_TRANSPOSE + 1
-X_QUANTISE = X_COPY + 1
-FX_MULTIPLY = SLOTS_PER_BATCH + X_QUANTISE + 2
-W_PIECES = 8
-W_REGROUP = FX_MULTIPLY - W_PIECES - 1
-W_QUANTISE = W_REGROUP + 1
-FX_BIAS = FX_MULTIPLY + 1
-FX_QUANTISE = FX_BIAS + 1
-XM_TRANSPOSE = 8
+XM_TRANSPOSE = 0
 XM_COPY = XM_TRANSPOSE + 1
 PROJECT = XM_COPY + 1
 LOGITS = PROJECT + 1
@@ -50,6 +41,16 @@ NORMALISE = SPREAD_COPY + 2
 N_QUANTISE = NORMALISE + 1
 POOL = N_QUANTISE + 1
 OUT_COPY = POOL + 1
+FX_QUANTISE = N_QUANTISE
+FX_BIAS = FX_QUANTISE - 1
+FX_MULTIPLY = FX_BIAS - 1
+FIRST_X = 2
+X_COPY = 1
+X_QUANTISE = 2
+LATER_X = FX_MULTIPLY - 1 - X_QUANTISE - (SLOTS_PER_BATCH - 1)
+W_PIECES = 8
+W_REGROUP = 7
+W_QUANTISE = W_REGROUP + 1
 STEPS = UNITS + OUT_COPY
 
 FLOPS = 2 * (B * N * C * E + B * N * H * D * S + B * H * S * D * N)
@@ -72,6 +73,7 @@ def tile_physicsattentionbase_pa_t_kernel(tc, x, x_mid, Wfx, bfx, Wslice, bslice
         x_rows = {}
         xm_rows = {}
         transposed = {}
+        first_x = {}
         x_grouped = {}
         x_codes = {}
         x_scales = {}
@@ -112,23 +114,24 @@ def tile_physicsattentionbase_pa_t_kernel(tc, x, x_mid, Wfx, bfx, Wslice, bslice
                 in_=x[b, g * K_PASS : (g + 1) * K_PASS, :].rearrange("(p t) c -> p (t c)", t=PACK),
             )
 
-        def load_x_mid(b, g):
-            xm_rows[b, g] = rows.tile([P, PACK, E], BF16, name="xm_rows", tag="xm_rows", bufs=4)
+        def load_x_mid(b, g, heads=(0, H)):
+            first, end = heads
+            if first == 0:
+                xm_rows[b, g] = rows.tile([P, PACK, E], BF16, name="xm_rows", tag="xm_rows", bufs=4)
             nc.sync.dma_start(
-                out=xm_rows[b, g][:].rearrange("p t e -> p (t e)"),
-                in_=x_mid[b, g * K_PASS : (g + 1) * K_PASS].rearrange("(p t) h d -> p (t h d)", t=PACK),
+                out=xm_rows[b, g][:, :, first * D : end * D],
+                in_=x_mid[b, g * K_PASS : (g + 1) * K_PASS, first:end, :].rearrange("(p t) h d -> p t (h d)", t=PACK),
             )
 
         def load_rows(step):
-            if step % SLOTS_PER_BLOCK == 0:
-                b, g = divmod(step // SLOTS_PER_BLOCK + 2, BLOCKS)
-                if b < B:
+            for n in range(BLOCKS + 1, B * BLOCKS):
+                b, g = divmod(n, BLOCKS)
+                if step == max(FIRST_X + SLOTS_PER_BLOCK // 2, UNITS_PER_BATCH * b + LATER_X + SLOTS_PER_BLOCK * (g - 2)):
                     load_x(b, g)
-            if step >= XM_TRANSPOSE and (step - XM_TRANSPOSE) % UNITS_PER_BATCH == 0:
-                b = (step - XM_TRANSPOSE) // UNITS_PER_BATCH + 1
-                if b < B:
-                    for g in range(BLOCKS):
-                        load_x_mid(b, g)
+            b, i = divmod(step, UNITS_PER_BATCH)
+            if i == 6 and b + 1 < B:
+                for g in range(BLOCKS):
+                    load_x_mid(b + 1, g)
 
         temp_bc = const.tile([P, H], BF16)
         nc.scalar.dma_start(out=temp_bc[:], in_=temp.rearrange("a b h c -> (a b h c)").partition_broadcast(P))
@@ -137,11 +140,11 @@ def tile_physicsattentionbase_pa_t_kernel(tc, x, x_mid, Wfx, bfx, Wslice, bslice
         wslice_sb = const.tile([P, S], BF16)
         nc.scalar.dma_start(out=wslice_sb[:], in_=Wslice)
         bfx_bc = const.tile([P, E], BF16)
-        nc.scalar.dma_start(out=bfx_bc[:], in_=bfx.partition_broadcast(P))
 
-        load_x(0, 0)
-        load_x_mid(0, 0)
-        load_x_mid(0, 1)
+        for heads in ((0, 2), (2, 4)):
+            for g in range(BLOCKS):
+                load_x_mid(0, g, heads)
+            load_x(0, heads[0] // 2)
         w_rows = []
         for k in range(C_PASSES):
             w_rows_k = rows.tile([P, PACK, E], BF16, tag="w_rows")
@@ -150,7 +153,10 @@ def tile_physicsattentionbase_pa_t_kernel(tc, x, x_mid, Wfx, bfx, Wslice, bslice
                 in_=Wfx[k * K_PASS : (k + 1) * K_PASS, :].rearrange("(u q e) c -> q u (e c)", u=2, e=2),
             )
             w_rows.append(w_rows_k)
-        load_x(0, 1)
+        for g in range(BLOCKS):
+            load_x_mid(0, g, (4, H))
+        nc.sync.dma_start(out=bfx_bc[:], in_=bfx.partition_broadcast(P))
+        load_x(1, 0)
 
         ident_f32 = const.tile([P, P], F32)
         make_identity(nc, ident_f32[:])
@@ -173,7 +179,7 @@ def tile_physicsattentionbase_pa_t_kernel(tc, x, x_mid, Wfx, bfx, Wslice, bslice
         def regroup_w(piece):
             if not 0 <= piece < W_PIECES:
                 return
-            k, part = divmod(piece, W_PIECES // C_PASSES)
+            part, k = divmod(piece, C_PASSES)
             w_grouped[piece] = work.tile([P, W_COLS, PACK], BF16, name="w_grouped", tag="w_grouped", align_bytes=64)
             nc.vector.tensor_copy(
                 out=w_grouped[piece][:],
@@ -183,7 +189,7 @@ def tile_physicsattentionbase_pa_t_kernel(tc, x, x_mid, Wfx, bfx, Wslice, bslice
         def quantise_w(piece):
             if not 0 <= piece < W_PIECES:
                 return
-            k, part = divmod(piece, W_PIECES // C_PASSES)
+            part, k = divmod(piece, C_PASSES)
             nc.vector.quantize_mx(
                 out=w_codes[:, k, part * W_COLS : (part + 1) * W_COLS].bitcast(FP8X4),
                 scales=w_scales[:, k, part * W_COLS : (part + 1) * W_COLS],
@@ -193,26 +199,35 @@ def tile_physicsattentionbase_pa_t_kernel(tc, x, x_mid, Wfx, bfx, Wslice, bslice
         MASS_REGIONS = 4
         mass_ps = ps_mass.tile([P, MASS_REGIONS, P], F32)
 
+        def later_slot(step):
+            b, i = divmod(step - LATER_X, SLOTS_PER_BATCH)
+            return b * SLOTS_PER_BATCH + i if 1 <= b < B else None
+
+        def transpose_slot(i, pairs):
+            block, rest = divmod(i, SLOTS_PER_BLOCK)
+            b, g = divmod(block, BLOCKS)
+            t, k = divmod(rest, C_PASSES)
+            words = x_rows[b, g][:, t, :].bitcast(F32)
+            for half in range(2):
+                first = (k * 2 + half) * P
+                nc.tensor.transpose(pairs[:, half * P : (half + 1) * P], words[:, first : first + P], ident_f32[:])
+
         def transpose_rows(step):
             u = step - XM_TRANSPOSE
-            i = step - X_TRANSPOSE
-            if not (is_unit(u) or 0 <= i < SLOTS):
-                return
-            bank = ps_tr.tile([P, 2 * PACK * P], BF16, name="transposed", tag="transposed")
-            transposed[step] = bank
+            i = later_slot(step)
+            if is_unit(u) or i is not None:
+                transposed[step] = ps_tr.tile([P, 2 * PACK * P], BF16, name="transposed", tag="transposed")
             if is_unit(u):
                 b, h, g = unit(u)
                 for t in range(PACK):
-                    nc.tensor.transpose(bank[:, t * P : (t + 1) * P], xm_rows[b, g][:, t, h * D : (h + 1) * D], ident_bf[:])
-            if 0 <= i < SLOTS:
-                block, rest = divmod(i, SLOTS_PER_BLOCK)
-                b, g = divmod(block, BLOCKS)
-                t, k = divmod(rest, C_PASSES)
-                words = x_rows[b, g][:, t, :].bitcast(F32)
-                pairs = bank[:, PACK * P :].bitcast(F32)
-                for half in range(2):
-                    first = (k * 2 + half) * P
-                    nc.tensor.transpose(pairs[:, half * P : (half + 1) * P], words[:, first : first + P], ident_f32[:])
+                    nc.tensor.transpose(transposed[step][:, t * P : (t + 1) * P], xm_rows[b, g][:, t, h * D : (h + 1) * D], ident_bf[:])
+            if i is not None:
+                transpose_slot(i, transposed[step][:, PACK * P :].bitcast(F32))
+            pair = step - FIRST_X
+            if 0 <= pair < SLOTS_PER_BATCH // 2:
+                first_x[pair] = ps_fx.tile([P, 2, 2 * P], F32, name="first_x", tag="fx_ps")
+                for j in range(2):
+                    transpose_slot(2 * pair + j, first_x[pair][:, j, :])
 
         def copy_transposed(step):
             u = step - XM_COPY
@@ -220,18 +235,27 @@ def tile_physicsattentionbase_pa_t_kernel(tc, x, x_mid, Wfx, bfx, Wslice, bslice
                 xm_t[u] = work.tile([P, PACK, P], BF16, name="xm_t", tag="xm_t", bufs=3)
                 bank = transposed[u + XM_TRANSPOSE]
                 nc.scalar.copy(out=xm_t[u][:].rearrange("d t p -> d (t p)"), in_=bank[:, : PACK * P])
-            i = step - X_COPY
-            if 0 <= i < SLOTS:
+            i = later_slot(step - X_COPY)
+            if i is not None:
                 if i % 2 == 0:
                     x_grouped[i // 2] = work.tile([P, 2, P, PACK], BF16, name="x_grouped", tag="x_grouped", bufs=3, align_bytes=64)
-                pairs = transposed[i + X_TRANSPOSE][:, PACK * P :].bitcast(F32)
+                pairs = transposed[step - X_COPY][:, PACK * P :].bitcast(F32)
                 nc.scalar.copy(
                     out=x_grouped[i // 2][:, i % 2].bitcast(F32),
                     in_=pairs.rearrange("q (u p) -> q p u", u=2),
                 )
+            pair = step - FIRST_X - X_COPY
+            if 0 <= pair < SLOTS_PER_BATCH // 2:
+                x_grouped[pair] = work.tile([P, 2, P, PACK], BF16, name="x_grouped", tag="x_grouped", bufs=3, align_bytes=64)
+                nc.scalar.copy(
+                    out=x_grouped[pair][:].bitcast(F32),
+                    in_=first_x[pair][:].rearrange("q i (u p) -> q i p u", u=2),
+                )
 
-        def quantise_x(i):
-            if not (0 <= i < SLOTS and i % 2 == 1):
+        def quantise_x(step):
+            pair = step - FIRST_X - X_QUANTISE
+            i = 2 * pair + 1 if 0 <= pair < SLOTS_PER_BATCH // 2 else later_slot(step - X_QUANTISE)
+            if i is None or i % 2 == 0:
                 return
             b, slot = divmod(i, SLOTS_PER_BATCH)
             if slot == 1:
@@ -449,7 +473,7 @@ def tile_physicsattentionbase_pa_t_kernel(tc, x, x_mid, Wfx, bfx, Wslice, bslice
             add_mass(step - MASS)
             spread_inv_mass(step - INV_MASS)
             normalise(step - NORMALISE)
-            quantise_x(step - X_QUANTISE)
+            quantise_x(step)
             quantise_head(step - FX_QUANTISE, fx_grouped, fx_codes, fx_scales, "fx")
             quantise_head(step - N_QUANTISE, n_grouped, n_codes, n_scales, "n")
             quantise_w(step - W_QUANTISE)

@@ -19,39 +19,25 @@ PACK = 4
 K_PASS = P * PACK
 C_PASSES = C // K_PASS
 BLOCKS = N // K_PASS
-
-UNITS_PER_BATCH = H * BLOCKS
-UNITS = B * UNITS_PER_BATCH
-SLOTS_PER_BLOCK = PACK * C_PASSES
-SLOTS_PER_BATCH = BLOCKS * SLOTS_PER_BLOCK
-SLOTS = B * SLOTS_PER_BATCH
+HEADS = B * H
+ROW_TILES = BLOCKS * PACK
 
 XM_TRANSPOSE = 0
-XM_COPY = XM_TRANSPOSE + 1
-PROJECT = XM_COPY + 1
-LOGITS = PROJECT + 1
-ROW_MAX = LOGITS
-EXP = ROW_MAX + 2
-INV_SUM = EXP + 1
-SCALE = INV_SUM + 2
-MASS = SCALE + 1
-INV_MASS = MASS + 1
-SPREAD_COPY = INV_MASS + 1
-NORMALISE = SPREAD_COPY + 2
-N_QUANTISE = NORMALISE + 1
-POOL = N_QUANTISE + 1
-OUT_COPY = POOL + 1
-FX_QUANTISE = N_QUANTISE
-FX_BIAS = FX_QUANTISE - 1
-FX_MULTIPLY = FX_BIAS - 1
+PROJECT = 1
+SOFTMAX = 2
+SCALE = 3
+MASS = 4
+INV_MASS = 5
+NORMALISE = 6
+QUANTISE = 7
+FX = 7
+POOL = 8
 FIRST_X = 2
-X_COPY = 1
-X_QUANTISE = 2
-LATER_X = FX_MULTIPLY - 1 - X_QUANTISE - (SLOTS_PER_BATCH - 1)
+LATER_X = FX - ROW_TILES - 1
 W_PIECES = 8
-W_REGROUP = 7
-W_QUANTISE = W_REGROUP + 1
-STEPS = UNITS + OUT_COPY
+W_REGROUP = 4
+STEPS = HEADS + POOL
+VECTOR_SCALED = ((0, 3), (1, 3))
 
 FLOPS = 2 * (B * N * C * E + B * N * H * D * S + B * H * S * D * N)
 
@@ -63,20 +49,21 @@ def tile_physicsattentionbase_pa_t_kernel(tc, x, x_mid, Wfx, bfx, Wslice, bslice
         rows = stack.enter_context(tc.tile_pool(name="rows", bufs=2))
         work = stack.enter_context(tc.tile_pool(name="work", bufs=2))
         stats = stack.enter_context(tc.tile_pool(name="stats", bufs=3))
-        ps_tr = stack.enter_context(tc.psum_pool(name="ps_tr", bufs=2))
-        ps_proj = stack.enter_context(tc.psum_pool(name="ps_proj", bufs=2))
+        ps_xm = stack.enter_context(tc.psum_pool(name="ps_xm", bufs=1))
+        ps_x = stack.enter_context(tc.psum_pool(name="ps_x", bufs=1))
+        ps_proj0 = stack.enter_context(tc.psum_pool(name="ps_proj0", bufs=1))
+        ps_proj1 = stack.enter_context(tc.psum_pool(name="ps_proj1", bufs=2))
         ps_fx = stack.enter_context(tc.psum_pool(name="ps_fx", bufs=2))
-        ps_mass = stack.enter_context(tc.psum_pool(name="ps_mass", bufs=1))
-        ps_misc = stack.enter_context(tc.psum_pool(name="ps_misc", bufs=1))
+        ps_small = stack.enter_context(tc.psum_pool(name="ps_small", bufs=1))
         stack.enter_context(tc.manual_schedule())
 
         x_rows = {}
         xm_rows = {}
-        transposed = {}
-        first_x = {}
+        x_banks = {}
         x_grouped = {}
         x_codes = {}
         x_scales = {}
+        xm_bank = {}
         xm_t = {}
         proj_ps = {}
         w = {}
@@ -85,7 +72,6 @@ def tile_physicsattentionbase_pa_t_kernel(tc, x, x_mid, Wfx, bfx, Wslice, bslice
         inv_sum = {}
         mass = {}
         inv_mass = {}
-        spread_ps = {}
         inv_mass_bc = {}
         n_grouped = {}
         n_codes = {}
@@ -94,18 +80,9 @@ def tile_physicsattentionbase_pa_t_kernel(tc, x, x_mid, Wfx, bfx, Wslice, bslice
         fx_grouped = {}
         fx_codes = {}
         fx_scales = {}
-        out_ps = {}
 
-        def unit(u):
-            b, rest = divmod(u, UNITS_PER_BATCH)
-            h, g = divmod(rest, BLOCKS)
-            return b, h, g
-
-        def is_unit(u):
-            return 0 <= u < UNITS
-
-        def ends_head(u):
-            return is_unit(u) and u % BLOCKS == BLOCKS - 1
+        def is_head(i):
+            return 0 <= i < HEADS
 
         def load_x(b, g):
             x_rows[b, g] = rows.tile([P, PACK, C], BF16, name="x_rows", tag="x_rows", bufs=3)
@@ -114,24 +91,35 @@ def tile_physicsattentionbase_pa_t_kernel(tc, x, x_mid, Wfx, bfx, Wslice, bslice
                 in_=x[b, g * K_PASS : (g + 1) * K_PASS, :].rearrange("(p t) c -> p (t c)", t=PACK),
             )
 
-        def load_x_mid(b, g, heads=(0, H)):
+        def load_x_mid(b, heads=(0, H)):
             first, end = heads
-            if first == 0:
-                xm_rows[b, g] = rows.tile([P, PACK, E], BF16, name="xm_rows", tag="xm_rows", bufs=4)
+            for g in range(BLOCKS):
+                if first == 0:
+                    xm_rows[b, g] = rows.tile([P, PACK, E], BF16, name="xm_rows", tag="xm_rows", bufs=4)
+                nc.sync.dma_start(
+                    out=xm_rows[b, g][:, :, first * D : end * D],
+                    in_=x_mid[b, g * K_PASS : (g + 1) * K_PASS, first:end, :].rearrange("(p t) h d -> p t (h d)", t=PACK),
+                )
+
+        w_rows = []
+
+        def load_w():
+            w_rows_k = rows.tile([P, PACK, E], BF16, tag="w_rows")
+            k = len(w_rows)
             nc.sync.dma_start(
-                out=xm_rows[b, g][:, :, first * D : end * D],
-                in_=x_mid[b, g * K_PASS : (g + 1) * K_PASS, first:end, :].rearrange("(p t) h d -> p t (h d)", t=PACK),
+                out=w_rows_k[:].rearrange("q (u e) c -> q u (e c)", u=2),
+                in_=Wfx[k * K_PASS : (k + 1) * K_PASS, :].rearrange("(u q e) c -> q u (e c)", u=2, e=2),
             )
+            w_rows.append(w_rows_k)
 
         def load_rows(step):
             for n in range(BLOCKS + 1, B * BLOCKS):
                 b, g = divmod(n, BLOCKS)
-                if step == max(FIRST_X + SLOTS_PER_BLOCK // 2, UNITS_PER_BATCH * b + LATER_X + SLOTS_PER_BLOCK * (g - 2)):
+                if step == max(FIRST_X + 2, H * b + LATER_X + PACK * (g - 2)):
                     load_x(b, g)
-            b, i = divmod(step, UNITS_PER_BATCH)
-            if i == 6 and b + 1 < B:
-                for g in range(BLOCKS):
-                    load_x_mid(b + 1, g)
+            b, h = divmod(step, H)
+            if h == 3 and b + 1 < B:
+                load_x_mid(b + 1)
 
         temp_bc = const.tile([P, H], BF16)
         nc.scalar.dma_start(out=temp_bc[:], in_=temp.rearrange("a b h c -> (a b h c)").partition_broadcast(P))
@@ -141,20 +129,14 @@ def tile_physicsattentionbase_pa_t_kernel(tc, x, x_mid, Wfx, bfx, Wslice, bslice
         nc.scalar.dma_start(out=wslice_sb[:], in_=Wslice)
         bfx_bc = const.tile([P, E], BF16)
 
-        for heads in ((0, 2), (2, 4)):
-            for g in range(BLOCKS):
-                load_x_mid(0, g, heads)
-            load_x(0, heads[0] // 2)
-        w_rows = []
-        for k in range(C_PASSES):
-            w_rows_k = rows.tile([P, PACK, E], BF16, tag="w_rows")
-            nc.sync.dma_start(
-                out=w_rows_k[:].rearrange("q (u e) c -> q u (e c)", u=2),
-                in_=Wfx[k * K_PASS : (k + 1) * K_PASS, :].rearrange("(u q e) c -> q u (e c)", u=2, e=2),
-            )
-            w_rows.append(w_rows_k)
-        for g in range(BLOCKS):
-            load_x_mid(0, g, (4, H))
+        load_x_mid(0, (0, 2))
+        load_x_mid(0, (2, 4))
+        load_x(0, 0)
+        load_x(0, 1)
+        load_x_mid(0, (4, 6))
+        load_w()
+        load_w()
+        load_x_mid(0, (6, H))
         nc.sync.dma_start(out=bfx_bc[:], in_=bfx.partition_broadcast(P))
         load_x(1, 0)
 
@@ -176,19 +158,19 @@ def tile_physicsattentionbase_pa_t_kernel(tc, x, x_mid, Wfx, bfx, Wslice, bslice
         w_grouped = {}
         W_COLS = C_PASSES * E // W_PIECES
 
+        def pieces(step):
+            first = 2 * (step - W_REGROUP)
+            return range(first, first + 2) if 0 <= first < W_PIECES else ()
+
         def regroup_w(piece):
-            if not 0 <= piece < W_PIECES:
-                return
             part, k = divmod(piece, C_PASSES)
-            w_grouped[piece] = work.tile([P, W_COLS, PACK], BF16, name="w_grouped", tag="w_grouped", align_bytes=64)
+            w_grouped[piece] = work.tile([P, W_COLS, PACK], BF16, name="w_grouped", tag="w_grouped", bufs=4, align_bytes=64)
             nc.vector.tensor_copy(
                 out=w_grouped[piece][:],
                 in_=w_rows[k][:, :, part * W_COLS : (part + 1) * W_COLS].rearrange("q j c -> q c j"),
             )
 
         def quantise_w(piece):
-            if not 0 <= piece < W_PIECES:
-                return
             part, k = divmod(piece, C_PASSES)
             nc.vector.quantize_mx(
                 out=w_codes[:, k, part * W_COLS : (part + 1) * W_COLS].bitcast(FP8X4),
@@ -196,285 +178,297 @@ def tile_physicsattentionbase_pa_t_kernel(tc, x, x_mid, Wfx, bfx, Wslice, bslice
                 in_=w_grouped[piece][:].rearrange("q c j -> q (c j)"),
             )
 
-        MASS_REGIONS = 4
-        mass_ps = ps_mass.tile([P, MASS_REGIONS, P], F32)
+        small = ps_small.tile([P, 4, P], F32)
+        SPREAD, POOLED = 2, 3
 
-        def later_slot(step):
-            b, i = divmod(step - LATER_X, SLOTS_PER_BATCH)
-            return b * SLOTS_PER_BATCH + i if 1 <= b < B else None
+        def row_tiles(step):
+            if 0 <= step - FIRST_X < ROW_TILES // 2:
+                return [(0, 2 * (step - FIRST_X) + i) for i in range(2)]
+            b, r = divmod(step - LATER_X, H)
+            return [(b, r)] if 1 <= b < B else []
 
-        def transpose_slot(i, pairs):
-            block, rest = divmod(i, SLOTS_PER_BLOCK)
-            b, g = divmod(block, BLOCKS)
-            t, k = divmod(rest, C_PASSES)
-            words = x_rows[b, g][:, t, :].bitcast(F32)
-            for half in range(2):
-                first = (k * 2 + half) * P
-                nc.tensor.transpose(pairs[:, half * P : (half + 1) * P], words[:, first : first + P], ident_f32[:])
+        def transpose_x(step):
+            x_banks[step] = []
+            for b, r in row_tiles(step):
+                g, t = divmod(r, PACK)
+                if b == 0:
+                    bank = ps_fx.tile([P, C_PASSES, 2 * P], F32, name="first_x", tag="fx_ps")
+                else:
+                    bank = ps_x.tile([P, C_PASSES, 2 * P], F32, name="later_x", tag="later_x")
+                x_banks[step].append((b, r, bank))
+                words = x_rows[b, g][:, t, :].bitcast(F32)
+                for k in range(C_PASSES):
+                    for half in range(2):
+                        first = (k * 2 + half) * P
+                        nc.tensor.transpose(bank[:, k, half * P : (half + 1) * P], words[:, first : first + P], ident_f32[:])
 
-        def transpose_rows(step):
-            u = step - XM_TRANSPOSE
-            i = later_slot(step)
-            if is_unit(u) or i is not None:
-                transposed[step] = ps_tr.tile([P, 2 * PACK * P], BF16, name="transposed", tag="transposed")
-            if is_unit(u):
-                b, h, g = unit(u)
-                for t in range(PACK):
-                    nc.tensor.transpose(transposed[step][:, t * P : (t + 1) * P], xm_rows[b, g][:, t, h * D : (h + 1) * D], ident_bf[:])
-            if i is not None:
-                transpose_slot(i, transposed[step][:, PACK * P :].bitcast(F32))
-            pair = step - FIRST_X
-            if 0 <= pair < SLOTS_PER_BATCH // 2:
-                first_x[pair] = ps_fx.tile([P, 2, 2 * P], F32, name="first_x", tag="fx_ps")
-                for j in range(2):
-                    transpose_slot(2 * pair + j, first_x[pair][:, j, :])
-
-        def copy_transposed(step):
-            u = step - XM_COPY
-            if is_unit(u):
-                xm_t[u] = work.tile([P, PACK, P], BF16, name="xm_t", tag="xm_t", bufs=3)
-                bank = transposed[u + XM_TRANSPOSE]
-                nc.scalar.copy(out=xm_t[u][:].rearrange("d t p -> d (t p)"), in_=bank[:, : PACK * P])
-            i = later_slot(step - X_COPY)
-            if i is not None:
-                if i % 2 == 0:
-                    x_grouped[i // 2] = work.tile([P, 2, P, PACK], BF16, name="x_grouped", tag="x_grouped", bufs=3, align_bytes=64)
-                pairs = transposed[step - X_COPY][:, PACK * P :].bitcast(F32)
+        def copy_x(step):
+            for b, r, bank in x_banks.get(step - 1, []):
+                x_grouped[b, r] = work.tile([P, C_PASSES, P, PACK], BF16, name="x_grouped", tag="x_grouped", bufs=4, align_bytes=64)
                 nc.scalar.copy(
-                    out=x_grouped[i // 2][:, i % 2].bitcast(F32),
-                    in_=pairs.rearrange("q (u p) -> q p u", u=2),
-                )
-            pair = step - FIRST_X - X_COPY
-            if 0 <= pair < SLOTS_PER_BATCH // 2:
-                x_grouped[pair] = work.tile([P, 2, P, PACK], BF16, name="x_grouped", tag="x_grouped", bufs=3, align_bytes=64)
-                nc.scalar.copy(
-                    out=x_grouped[pair][:].bitcast(F32),
-                    in_=first_x[pair][:].rearrange("q i (u p) -> q i p u", u=2),
+                    out=x_grouped[b, r][:].bitcast(F32),
+                    in_=bank[:].rearrange("q k (u p) -> q k p u", u=2),
                 )
 
         def quantise_x(step):
-            pair = step - FIRST_X - X_QUANTISE
-            i = 2 * pair + 1 if 0 <= pair < SLOTS_PER_BATCH // 2 else later_slot(step - X_QUANTISE)
-            if i is None or i % 2 == 0:
+            for b, r, bank in x_banks.get(step - 1, []):
+                if r == 0:
+                    x_codes[b] = work.tile([P, ROW_TILES, C_PASSES, P], U32, name="x_codes", tag="x_codes", bufs=3, align_bytes=64)
+                    x_scales[b] = work.tile([P, ROW_TILES, C_PASSES, P], U8, name="x_scales", tag="x_scales", bufs=3, align_bytes=64)
+                nc.vector.quantize_mx(
+                    out=x_codes[b][:, r].rearrange("q k p -> q (k p)").bitcast(FP8X4),
+                    scales=x_scales[b][:, r].rearrange("q k p -> q (k p)"),
+                    in_=x_grouped[b, r][:].rearrange("q k p j -> q (k p j)"),
+                )
+
+        def transpose_x_mid(i):
+            if not is_head(i):
                 return
-            b, slot = divmod(i, SLOTS_PER_BATCH)
-            if slot == 1:
-                x_codes[b] = work.tile([P, SLOTS_PER_BATCH, P], U32, name="x_codes", tag="x_codes", bufs=3, align_bytes=64)
-                x_scales[b] = work.tile([P, SLOTS_PER_BATCH, P], U8, name="x_scales", tag="x_scales", bufs=3, align_bytes=64)
-            nc.vector.quantize_mx(
-                out=x_codes[b][:, slot - 1 : slot + 1].rearrange("q i p -> q (i p)").bitcast(FP8X4),
-                scales=x_scales[b][:, slot - 1 : slot + 1].rearrange("q i p -> q (i p)"),
-                in_=x_grouped[i // 2][:].rearrange("q i p j -> q (i p j)"),
+            b, h = divmod(i, H)
+            xm_bank[i] = ps_xm.tile([P, BLOCKS, PACK, P], BF16, name="xm_bank", tag="xm_bank")
+            for g in range(BLOCKS):
+                for t in range(PACK):
+                    nc.tensor.transpose(xm_bank[i][:, g, t, :], xm_rows[b, g][:, t, h * D : (h + 1) * D], ident_bf[:])
+
+        def copy_x_mid(i):
+            if not is_head(i):
+                return
+            xm_t[i] = work.tile([P, BLOCKS, PACK, P], BF16, name="xm_t", tag="xm_t")
+            nc.scalar.copy(
+                out=xm_t[i][:].rearrange("d g t p -> d (g t p)"), in_=xm_bank[i][:].rearrange("d g t p -> d (g t p)")
             )
 
-        def project(u):
-            if not is_unit(u):
-                return
-            proj_ps[u] = ps_proj.tile([P, PACK, S], F32, name="proj_ps", tag="proj_ps")
-            for t in range(PACK):
-                nc.tensor.matmul(out=proj_ps[u][:, t, :], lhsT=xm_t[u][:, t, :], rhs=wslice_sb[:], start=True, stop=True)
+        def bias_in_psum(i):
+            return i < HEADS - 1
 
-        def logits(u):
-            if not is_unit(u):
+        def project(i):
+            if not is_head(i):
                 return
-            b, h, g = unit(u)
-            if g == 0:
-                w[u // BLOCKS] = work.tile([P, BLOCKS, PACK, S], F32, name="w", tag="w", bufs=8)
+            proj_ps[i, 0] = ps_proj0.tile([P, PACK, S], F32, name="proj0", tag="proj0")
+            proj_ps[i, 1] = ps_proj1.tile([P, PACK, S], F32, name="proj1", tag="proj1")
+            for g in range(BLOCKS):
+                with_bias = g == 1 and bias_in_psum(i)
+                for t in range(PACK):
+                    region = proj_ps[i, g][:, t, :]
+                    if with_bias:
+                        nc.tensor.matmul(out=region, lhsT=ident_bf[:], rhs=bslice_bc[:], start=True, stop=False)
+                    nc.tensor.matmul(out=region, lhsT=xm_t[i][:, g, t, :], rhs=wslice_sb[:], start=not with_bias, stop=True)
+
+        def logits(i, g):
+            b, h = divmod(i, H)
             nc.vector.scalar_tensor_tensor(
-                out=w[u // BLOCKS][:, g],
-                in0=proj_ps[u][:],
+                out=w[i][:, g],
+                in0=proj_ps[i, g][:],
                 scalar=inv_temp[:, h : h + 1],
                 in1=bias_over_temp[:, h, :].unsqueeze(1).to_broadcast([P, PACK, S]),
                 op0=ALU.mult,
                 op1=ALU.add,
             )
 
-        def row_max(u):
-            if not ends_head(u):
-                return
-            head = u // BLOCKS
-            neg_max[head] = stats.tile([P, BLOCKS, PACK], F32, name="neg_max", tag="neg_max")
-            nc.vector.tensor_reduce(out=neg_max[head][:], in_=w[head][:], axis=AXIS_X, op=ALU.max, negate=True)
+        def row_max(i, g, source):
+            nc.vector.tensor_reduce(out=neg_max[i, g][:], in_=source, axis=AXIS_X, op=ALU.max, negate=True)
 
-        def exponentials(u):
-            if not is_unit(u):
+        def softmax_begin(i):
+            if not is_head(i):
                 return
-            head, g = divmod(u, BLOCKS)
-            if g == 0:
-                sum_exp[head] = stats.tile([P, BLOCKS, PACK], F32, name="sum_exp", tag="sum_exp")
-            for t in range(PACK):
-                nc.scalar.activation(
-                    out=w[head][:, g, t, :],
-                    in_=w[head][:, g, t, :],
-                    func=ACT.Exp,
-                    bias=neg_max[head][:, g, t : t + 1],
-                    scale=1.0,
-                    accum_out=sum_exp[head][:, g, t : t + 1],
-                )
+            b, h = divmod(i, H)
+            w[i] = work.tile([P, BLOCKS, PACK, S], F32, name="w", tag="w", bufs=7)
+            for g in range(BLOCKS):
+                neg_max[i, g] = stats.tile([P, PACK], F32, name="neg_max", tag="neg_max%d" % g)
+            if bias_in_psum(i):
+                raw = stats.tile([P, PACK], F32, tag="raw_max")
+                nc.vector.tensor_reduce(out=raw[:], in_=proj_ps[i, 1][:], axis=AXIS_X, op=ALU.max, negate=True)
+                logits(i, 0)
+                nc.vector.tensor_scalar_mul(out=neg_max[i, 1][:], in0=raw[:], scalar1=inv_temp[:, h : h + 1])
+            else:
+                logits(i, 1)
+                logits(i, 0)
+                row_max(i, 1, w[i][:, 1])
 
-        def invert_sums(u):
-            if not ends_head(u):
-                return
-            head = u // BLOCKS
-            inv_sum[head] = stats.tile([P, BLOCKS, PACK], F32, name="inv_sum", tag="inv_sum")
-            nc.vector.reciprocal(out=inv_sum[head][:], in_=sum_exp[head][:])
+        def softmax_end(i):
+            if is_head(i):
+                row_max(i, 0, w[i][:, 0])
 
-        def scale_rows(u):
-            if not is_unit(u):
+        def exponentials(i):
+            if not is_head(i):
                 return
-            head, g = divmod(u, BLOCKS)
-            for t in range(PACK):
-                nc.scalar.activation(
-                    out=w[head][:, g, t, :], in_=w[head][:, g, t, :], func=ACT.Copy, scale=inv_sum[head][:, g, t : t + 1]
-                )
-
-        def add_mass(u):
-            if not is_unit(u):
-                return
-            b, h, g = unit(u)
-            for t in range(PACK):
-                nc.tensor.matmul(
-                    out=mass_ps[:, h % MASS_REGIONS, :],
-                    lhsT=w[u // BLOCKS][:, g, t, :],
-                    rhs=ident_f32[:],
-                    is_transpose=True,
-                    start=(g == 0 and t == 0),
-                    stop=(g == BLOCKS - 1 and t == PACK - 1),
-                )
-
-        def sum_mass(u):
-            if not ends_head(u):
-                return
-            b, h, g = unit(u)
-            mass[u] = stats.tile([P, 1], F32, name="mass", tag="mass")
-            unread = stats.tile([P, P], F32, tag="unread")
-            nc.scalar.activation(out=unread[:], in_=mass_ps[:, h % MASS_REGIONS, :], func=ACT.Copy, accum_out=mass[u][:])
-
-        def invert_mass(u):
-            if not ends_head(u):
-                return
-            mass_eps = stats.tile([P, 1], F32, tag="mass_eps")
-            nc.vector.tensor_scalar_add(out=mass_eps[:], in0=mass[u][:], scalar1=0.01)
-            inv_mass[u] = stats.tile([P, 1], F32, name="inv_mass", tag="inv_mass")
-            nc.vector.reciprocal(out=inv_mass[u][:], in_=mass_eps[:])
-
-        def spread_inv_mass(u):
-            if not ends_head(u):
-                return
-            spread_ps[u] = ps_misc.tile([P, S], F32, name="spread_ps", tag="misc")
-            nc.tensor.transpose(spread_ps[u][:], inv_mass[u][:].to_broadcast([P, P]), ident_f32[:])
-
-        def copy_spread(u):
-            if not ends_head(u):
-                return
-            inv_mass_bc[u] = stats.tile([P, S], F32, name="inv_mass_bc", tag="inv_mass_bc")
-            nc.scalar.copy(out=inv_mass_bc[u][:], in_=spread_ps[u][:])
-
-        def normalise(u):
-            if not is_unit(u):
-                return
-            head, g = divmod(u, BLOCKS)
-            if g == 0:
-                n_grouped[head] = work.tile([P, BLOCKS, S, PACK], BF16, name="n_grouped", tag="n_grouped", bufs=3, align_bytes=64)
-            head_end = u - g + BLOCKS - 1
-            nc.gpsimd.tensor_tensor(
-                out=n_grouped[head][:, g],
-                in0=w[head][:, g].rearrange("p t s -> p s t"),
-                in1=inv_mass_bc[head_end][:].unsqueeze(2).to_broadcast([P, S, PACK]),
-                op=ALU.mult,
-            )
-
-        def quantise_head(u, grouped, codes, scales, name):
-            if not ends_head(u):
-                return
-            b, i = divmod(u, UNITS_PER_BATCH)
-            if i == BLOCKS - 1:
-                codes[b] = work.tile([P, UNITS_PER_BATCH, P], U32, name=name + "_codes", tag=name + "_codes", align_bytes=64)
-                scales[b] = work.tile([P, UNITS_PER_BATCH, P], U8, name=name + "_scales", tag=name + "_scales", align_bytes=64)
-            nc.vector.quantize_mx(
-                out=codes[b][:, i - BLOCKS + 1 : i + 1].rearrange("p g c -> p (g c)").bitcast(FP8X4),
-                scales=scales[b][:, i - BLOCKS + 1 : i + 1].rearrange("p g c -> p (g c)"),
-                in_=grouped[u // BLOCKS][:].rearrange("p g c t -> p (g c t)"),
-            )
-
-        def multiply_features(u):
-            if not is_unit(u):
-                return
-            b, h, g = unit(u)
-            fx_ps[u] = ps_fx.tile([P, PACK, D], F32, name="fx_ps", tag="fx_ps")
-            for t in range(PACK):
-                for k in range(C_PASSES):
-                    i = (g * PACK + t) * C_PASSES + k
-                    nc.tensor.matmul_mx(
-                        out=fx_ps[u][:, t, :],
-                        lhsT=x_codes[b][:, i, :].bitcast(FP8X4),
-                        lhsT_scale=x_scales[b][:, i, :],
-                        rhs=w_codes[:, k, h * D : (h + 1) * D].bitcast(FP8X4),
-                        rhs_scale=w_scales[:, k, h * D : (h + 1) * D],
-                        start=(k == 0),
-                        stop=(k == C_PASSES - 1),
+            b, h = divmod(i, H)
+            sum_exp[i] = stats.tile([P, BLOCKS, PACK], F32, name="sum_exp", tag="sum_exp")
+            for g in (1, 0):
+                from_psum = g == 1 and bias_in_psum(i)
+                for t in range(PACK):
+                    nc.scalar.activation(
+                        out=w[i][:, g, t, :],
+                        in_=proj_ps[i, g][:, t, :] if from_psum else w[i][:, g, t, :],
+                        func=ACT.Exp,
+                        bias=neg_max[i, g][:, t : t + 1],
+                        scale=inv_temp[:, h : h + 1] if from_psum else 1.0,
+                        accum_out=sum_exp[i][:, g, t : t + 1],
                     )
 
-        def add_feature_bias(u):
-            if not is_unit(u):
+        def invert_sums(i):
+            if not is_head(i):
                 return
-            b, h, g = unit(u)
+            inv_sum[i] = stats.tile([P, BLOCKS, PACK], F32, name="inv_sum", tag="inv_sum")
+            nc.vector.reciprocal(out=inv_sum[i][:], in_=sum_exp[i][:])
+
+        def scale_on_vector(i, g, t):
+            if is_head(i):
+                nc.vector.tensor_scalar_mul(out=w[i][:, g, t, :], in0=w[i][:, g, t, :], scalar1=inv_sum[i][:, g, t : t + 1])
+
+        def scale_on_scalar(i):
+            if not is_head(i):
+                return
+            for g in range(BLOCKS):
+                for t in range(PACK):
+                    if (g, t) not in VECTOR_SCALED:
+                        nc.scalar.activation(
+                            out=w[i][:, g, t, :], in_=w[i][:, g, t, :], func=ACT.Copy, scale=inv_sum[i][:, g, t : t + 1]
+                        )
+
+        def add_mass(i):
+            if not is_head(i):
+                return
+            for g in range(BLOCKS):
+                for t in range(PACK):
+                    nc.tensor.matmul(
+                        out=small[:, i % 2, :],
+                        lhsT=w[i][:, g, t, :],
+                        rhs=ident_f32[:],
+                        is_transpose=True,
+                        start=(g == 0 and t == 0),
+                        stop=(g == BLOCKS - 1 and t == PACK - 1),
+                    )
+
+        def sum_mass(i):
+            if not is_head(i):
+                return
+            mass[i] = stats.tile([P, 1], F32, name="mass", tag="mass")
+            unread = stats.tile([P, P], F32, tag="unread")
+            nc.scalar.activation(out=unread[:], in_=small[:, i % 2, :], func=ACT.Copy, accum_out=mass[i][:])
+
+        def invert_mass(i):
+            if not is_head(i):
+                return
+            mass_eps = stats.tile([P, 1], F32, tag="mass_eps")
+            nc.vector.tensor_scalar_add(out=mass_eps[:], in0=mass[i][:], scalar1=0.01)
+            inv_mass[i] = stats.tile([P, 1], F32, name="inv_mass", tag="inv_mass")
+            nc.vector.reciprocal(out=inv_mass[i][:], in_=mass_eps[:])
+
+        def spread_inv_mass(i):
+            if is_head(i):
+                nc.tensor.transpose(small[:, SPREAD, :], inv_mass[i][:].to_broadcast([P, P]), ident_f32[:])
+
+        def copy_spread(i):
+            if not is_head(i):
+                return
+            inv_mass_bc[i] = stats.tile([P, S], F32, name="inv_mass_bc", tag="inv_mass_bc")
+            nc.scalar.copy(out=inv_mass_bc[i][:], in_=small[:, SPREAD, :])
+
+        def normalise(i):
+            if not is_head(i):
+                return
+            n_grouped[i] = work.tile([P, BLOCKS, S, PACK], BF16, name="n_grouped", tag="n_grouped", bufs=3, align_bytes=64)
+            for g in range(BLOCKS):
+                nc.gpsimd.tensor_tensor(
+                    out=n_grouped[i][:, g],
+                    in0=w[i][:, g].rearrange("p t s -> p s t"),
+                    in1=inv_mass_bc[i][:].unsqueeze(2).to_broadcast([P, S, PACK]),
+                    op=ALU.mult,
+                )
+
+        def quantise_head(i, grouped, codes, scales, name):
+            if not is_head(i):
+                return
+            codes[i] = work.tile([P, BLOCKS, P], U32, name=name + "_codes", tag=name + "_codes", bufs=3, align_bytes=64)
+            scales[i] = work.tile([P, BLOCKS, P], U8, name=name + "_scales", tag=name + "_scales", bufs=3, align_bytes=64)
+            nc.vector.quantize_mx(
+                out=codes[i][:].rearrange("p g c -> p (g c)").bitcast(FP8X4),
+                scales=scales[i][:].rearrange("p g c -> p (g c)"),
+                in_=grouped[i][:].rearrange("p g c t -> p (g c t)"),
+            )
+
+        def multiply_features(i):
+            if not is_head(i):
+                return
+            b, h = divmod(i, H)
+            for g in range(BLOCKS):
+                fx_ps[i, g] = ps_fx.tile([P, PACK, D], F32, name="fx_ps", tag="fx_ps")
+                for t in range(PACK):
+                    for k in range(C_PASSES):
+                        nc.tensor.matmul_mx(
+                            out=fx_ps[i, g][:, t, :],
+                            lhsT=x_codes[b][:, g * PACK + t, k, :].bitcast(FP8X4),
+                            lhsT_scale=x_scales[b][:, g * PACK + t, k, :],
+                            rhs=w_codes[:, k, h * D : (h + 1) * D].bitcast(FP8X4),
+                            rhs_scale=w_scales[:, k, h * D : (h + 1) * D],
+                            start=(k == 0),
+                            stop=(k == C_PASSES - 1),
+                        )
+
+        def add_feature_bias(i, g):
+            if not is_head(i):
+                return
+            b, h = divmod(i, H)
             if g == 0:
-                fx_grouped[u // BLOCKS] = work.tile([P, BLOCKS, D, PACK], BF16, name="fx_grouped", tag="fx_grouped", bufs=3, align_bytes=64)
+                fx_grouped[i] = work.tile([P, BLOCKS, D, PACK], BF16, name="fx_grouped", tag="fx_grouped", align_bytes=64)
             nc.vector.tensor_tensor(
-                out=fx_grouped[u // BLOCKS][:, g],
-                in0=fx_ps[u][:].rearrange("p t d -> p d t"),
+                out=fx_grouped[i][:, g],
+                in0=fx_ps[i, g][:].rearrange("p t d -> p d t"),
                 in1=bfx_bc[:, h * D : (h + 1) * D].unsqueeze(2).to_broadcast([P, D, PACK]),
                 op=ALU.add,
             )
 
-        def pool_points(u):
-            if not ends_head(u):
+        def pool_points(i):
+            if not is_head(i):
                 return
-            b, h, g = unit(u)
-            out_ps[u] = ps_misc.tile([P, D], F32, name="out_ps", tag="misc")
             for g in range(BLOCKS):
-                i = h * BLOCKS + g
                 nc.tensor.matmul_mx(
-                    out=out_ps[u][:],
-                    lhsT=n_codes[b][:, i, :].bitcast(FP8X4),
-                    lhsT_scale=n_scales[b][:, i, :],
-                    rhs=fx_codes[b][:, i, :].bitcast(FP8X4),
-                    rhs_scale=fx_scales[b][:, i, :],
+                    out=small[:, POOLED, :],
+                    lhsT=n_codes[i][:, g, :].bitcast(FP8X4),
+                    lhsT_scale=n_scales[i][:, g, :],
+                    rhs=fx_codes[i][:, g, :].bitcast(FP8X4),
+                    rhs_scale=fx_scales[i][:, g, :],
                     start=(g == 0),
                     stop=(g == BLOCKS - 1),
                 )
 
-        def copy_out(u):
-            if not ends_head(u):
+        def copy_out(i):
+            if not is_head(i):
                 return
-            b, h, g = unit(u)
             out_sb = work.tile([P, D], F32, tag="out_sb", bufs=4)
-            nc.scalar.copy(out=out_sb[:], in_=out_ps[u][:])
-            nc.scalar.dma_start(out=out[b, h], in_=out_sb[:])
+            nc.scalar.copy(out=out_sb[:], in_=small[:, POOLED, :])
+            nc.sync.dma_start(out=out[i // H, i % H], in_=out_sb[:])
 
         for step in range(STEPS):
             load_rows(step)
-            copy_spread(step - SPREAD_COPY)
-            copy_out(step - OUT_COPY)
+            copy_spread(step - NORMALISE)
+            copy_x_mid(step - PROJECT)
+            copy_x(step)
             sum_mass(step - INV_MASS)
-            copy_transposed(step)
-            project(step - PROJECT)
-            logits(step - LOGITS)
-            multiply_features(step - FX_MULTIPLY)
-            pool_points(step - POOL)
-            add_feature_bias(step - FX_BIAS)
+            softmax_begin(step - SOFTMAX)
+            invert_sums(step - SCALE)
+            softmax_end(step - SOFTMAX)
             invert_mass(step - INV_MASS)
-            row_max(step - ROW_MAX)
-            exponentials(step - EXP)
-            invert_sums(step - INV_SUM)
-            scale_rows(step - SCALE)
-            transpose_rows(step)
+            multiply_features(step - FX)
+            pool_points(step - POOL)
+            project(step - PROJECT)
+            add_feature_bias(step - FX, 0)
+            scale_on_vector(step - SCALE, *VECTOR_SCALED[0])
+            add_feature_bias(step - FX, 1)
+            scale_on_vector(step - SCALE, *VECTOR_SCALED[1])
+            scale_on_scalar(step - SCALE)
+            copy_out(step - POOL)
+            exponentials(step - SOFTMAX)
+            transpose_x_mid(step)
+            transpose_x(step)
             add_mass(step - MASS)
             spread_inv_mass(step - INV_MASS)
             normalise(step - NORMALISE)
             quantise_x(step)
-            quantise_head(step - FX_QUANTISE, fx_grouped, fx_codes, fx_scales, "fx")
-            quantise_head(step - N_QUANTISE, n_grouped, n_codes, n_scales, "n")
-            quantise_w(step - W_QUANTISE)
-            regroup_w(step - W_REGROUP)
+            quantise_head(step - QUANTISE, fx_grouped, fx_codes, fx_scales, "fx")
+            quantise_head(step - QUANTISE, n_grouped, n_codes, n_scales, "n")
+            for piece in pieces(step - 1):
+                quantise_w(piece)
+            for piece in pieces(step):
+                regroup_w(piece)

@@ -36,8 +36,8 @@ FIRST_X = 2
 LATER_X = FX - ROW_TILES - 1
 W_PIECES = 8
 W_REGROUP = 4
-STEPS = HEADS + POOL
-VECTOR_SCALED = ((0, 3), (1, 3))
+STEPS = HEADS + POOL + 1
+VECTOR_SCALED = ((0, 3), (1, 2), (1, 3))
 
 FLOPS = 2 * (B * N * C * E + B * N * H * D * S + B * H * S * D * N)
 
@@ -345,15 +345,13 @@ def tile_physicsattentionbase_pa_t_kernel(tc, x, x_mid, Wfx, bfx, Wslice, bslice
                 return
             mass[i] = stats.tile([P, 1], F32, name="mass", tag="mass")
             unread = stats.tile([P, P], F32, tag="unread")
-            nc.scalar.activation(out=unread[:], in_=small[:, i % 2, :], func=ACT.Copy, accum_out=mass[i][:])
+            nc.scalar.activation(out=unread[:], in_=small[:, i % 2, :], func=ACT.Copy, bias=0.01 / P, accum_out=mass[i][:])
 
         def invert_mass(i):
             if not is_head(i):
                 return
-            mass_eps = stats.tile([P, 1], F32, tag="mass_eps")
-            nc.vector.tensor_scalar_add(out=mass_eps[:], in0=mass[i][:], scalar1=0.01)
             inv_mass[i] = stats.tile([P, 1], F32, name="inv_mass", tag="inv_mass")
-            nc.vector.reciprocal(out=inv_mass[i][:], in_=mass_eps[:])
+            nc.vector.reciprocal(out=inv_mass[i][:], in_=mass[i][:])
 
         def spread_inv_mass(i):
             if is_head(i):
@@ -443,9 +441,10 @@ def tile_physicsattentionbase_pa_t_kernel(tc, x, x_mid, Wfx, bfx, Wslice, bslice
         for step in range(STEPS):
             load_rows(step)
             copy_spread(step - NORMALISE)
+            sum_mass(step - INV_MASS)
+            copy_out(step - POOL - 1)
             copy_x_mid(step - PROJECT)
             copy_x(step)
-            sum_mass(step - INV_MASS)
             softmax_begin(step - SOFTMAX)
             invert_sums(step - SCALE)
             softmax_end(step - SOFTMAX)
@@ -454,11 +453,10 @@ def tile_physicsattentionbase_pa_t_kernel(tc, x, x_mid, Wfx, bfx, Wslice, bslice
             pool_points(step - POOL)
             project(step - PROJECT)
             add_feature_bias(step - FX, 0)
-            scale_on_vector(step - SCALE, *VECTOR_SCALED[0])
             add_feature_bias(step - FX, 1)
-            scale_on_vector(step - SCALE, *VECTOR_SCALED[1])
+            for place in VECTOR_SCALED:
+                scale_on_vector(step - SCALE, *place)
             scale_on_scalar(step - SCALE)
-            copy_out(step - POOL)
             exponentials(step - SOFTMAX)
             transpose_x_mid(step)
             transpose_x(step)

@@ -369,9 +369,9 @@ def tile_physicsattentionbase_pa_t_kernel(tc, x, x_mid, Wfx, bfx, Wslice, bslice
             n_grouped[i] = work.tile([P, BLOCKS, S, PACK], BF16, name="n_grouped", tag="n_grouped", bufs=3, align_bytes=64)
             for g in range(BLOCKS):
                 nc.gpsimd.tensor_tensor(
-                    out=n_grouped[i][:, g],
-                    in0=w[i][:, g].rearrange("p t s -> p s t"),
-                    in1=inv_mass_bc[i][:].unsqueeze(2).to_broadcast([P, S, PACK]),
+                    out=n_grouped[i][:, g].rearrange("p (c i) t -> p c t i", i=4),
+                    in0=w[i][:, g].rearrange("p t (c i) -> p c t i", i=4),
+                    in1=inv_mass_bc[i][:].rearrange("p (c i) -> p c i", i=4).unsqueeze(2).to_broadcast([P, S // 4, PACK, 4]),
                     op=ALU.mult,
                 )
 

@@ -313,7 +313,7 @@ def tile_physicsattentionbase_pa_t_kernel(tc, x, x_mid, Wfx, bfx, Wslice, bslice
             nc.vector.reciprocal(out=inv_sum[i][:], in_=sum_exp[i][:])
 
         def scale_on_vector(i, g, t):
-            if is_head(i):
+            if is_head(i) and i < HEADS - 2:
                 nc.vector.tensor_scalar_mul(out=w[i][:, g, t, :], in0=w[i][:, g, t, :], scalar1=inv_sum[i][:, g, t : t + 1])
 
         def scale_on_scalar(i):
@@ -321,7 +321,7 @@ def tile_physicsattentionbase_pa_t_kernel(tc, x, x_mid, Wfx, bfx, Wslice, bslice
                 return
             for g in range(BLOCKS):
                 for t in range(PACK):
-                    if (g, t) not in VECTOR_SCALED:
+                    if (g, t) not in VECTOR_SCALED or i >= HEADS - 2:
                         nc.scalar.activation(
                             out=w[i][:, g, t, :], in_=w[i][:, g, t, :], func=ACT.Copy, scale=inv_sum[i][:, g, t : t + 1]
                         )
@@ -368,7 +368,8 @@ def tile_physicsattentionbase_pa_t_kernel(tc, x, x_mid, Wfx, bfx, Wslice, bslice
                 return
             n_grouped[i] = work.tile([P, BLOCKS, S, PACK], BF16, name="n_grouped", tag="n_grouped", bufs=3, align_bytes=64)
             for g in range(BLOCKS):
-                nc.gpsimd.tensor_tensor(
+                engine = nc.vector if g == 1 and i >= HEADS - 4 else nc.gpsimd
+                engine.tensor_tensor(
                     out=n_grouped[i][:, g].rearrange("p (c i) t -> p c t i", i=4),
                     in0=w[i][:, g].rearrange("p t (c i) -> p c t i", i=4),
                     in1=inv_mass_bc[i][:].rearrange("p (c i) -> p c i", i=4).unsqueeze(2).to_broadcast([P, S // 4, PACK, 4]),
@@ -451,6 +452,7 @@ def tile_physicsattentionbase_pa_t_kernel(tc, x, x_mid, Wfx, bfx, Wslice, bslice
             invert_mass(step - INV_MASS)
             multiply_features(step - FX)
             pool_points(step - POOL)
+            add_mass(step - MASS)
             project(step - PROJECT)
             add_feature_bias(step - FX, 0)
             add_feature_bias(step - FX, 1)
@@ -460,7 +462,6 @@ def tile_physicsattentionbase_pa_t_kernel(tc, x, x_mid, Wfx, bfx, Wslice, bslice
             exponentials(step - SOFTMAX)
             transpose_x_mid(step)
             transpose_x(step)
-            add_mass(step - MASS)
             spread_inv_mass(step - INV_MASS)
             normalise(step - NORMALISE)
             quantise_x(step)

@@ -30,14 +30,16 @@ MASS = 4
 INV_MASS = 5
 NORMALISE = 6
 QUANTISE = 7
-FX = 7
+FX = 6
 POOL = 8
-FIRST_X = 2
+FIRST_X = 1
 LATER_X = FX - ROW_TILES - 1
+X_LEAD = 6
 W_PIECES = 8
-W_REGROUP = 4
+W_REGROUP = 2
 STEPS = HEADS + POOL + 1
 VECTOR_SCALED = ((0, 3), (1, 2), (1, 3))
+GPSIMD_QUARTERS_AT_END = (2, 1, 1, 0)
 
 FLOPS = 2 * (B * N * C * E + B * N * H * D * S + B * H * S * D * N)
 
@@ -85,7 +87,7 @@ def tile_physicsattentionbase_pa_t_kernel(tc, x, x_mid, Wfx, bfx, Wslice, bslice
             return 0 <= i < HEADS
 
         def load_x(b, g):
-            x_rows[b, g] = rows.tile([P, PACK, C], BF16, name="x_rows", tag="x_rows", bufs=3)
+            x_rows[b, g] = rows.tile([P, PACK, C], BF16, name="x_rows", tag="x_rows", bufs=4)
             nc.sync.dma_start(
                 out=x_rows[b, g][:].rearrange("p t c -> p (t c)"),
                 in_=x[b, g * K_PASS : (g + 1) * K_PASS, :].rearrange("(p t) c -> p (t c)", t=PACK),
@@ -103,19 +105,21 @@ def tile_physicsattentionbase_pa_t_kernel(tc, x, x_mid, Wfx, bfx, Wslice, bslice
 
         w_rows = []
 
-        def load_w():
-            w_rows_k = rows.tile([P, PACK, E], BF16, tag="w_rows")
-            k = len(w_rows)
-            nc.sync.dma_start(
-                out=w_rows_k[:].rearrange("q (u e) c -> q u (e c)", u=2),
-                in_=Wfx[k * K_PASS : (k + 1) * K_PASS, :].rearrange("(u q e) c -> q u (e c)", u=2, e=2),
-            )
-            w_rows.append(w_rows_k)
+        def load_w(first, end):
+            for k in range(C_PASSES):
+                if first == 0:
+                    w_rows.append(rows.tile([P, PACK, E], BF16, name="w_rows", tag="w_rows"))
+                for u in range(2):
+                    start = k * K_PASS + u * 2 * P
+                    nc.sync.dma_start(
+                        out=w_rows[k][:, 2 * u : 2 * u + 2, first:end],
+                        in_=Wfx[start : start + 2 * P, first:end].rearrange("(q e) c -> q e c", e=2),
+                    )
 
         def load_rows(step):
             for n in range(BLOCKS + 1, B * BLOCKS):
                 b, g = divmod(n, BLOCKS)
-                if step == max(FIRST_X + 2, H * b + LATER_X + PACK * (g - 2)):
+                if step == max(FIRST_X + 3, H * b + LATER_X + PACK * g - X_LEAD):
                     load_x(b, g)
             b, h = divmod(step, H)
             if h == 3 and b + 1 < B:
@@ -130,14 +134,14 @@ def tile_physicsattentionbase_pa_t_kernel(tc, x, x_mid, Wfx, bfx, Wslice, bslice
         bfx_bc = const.tile([P, E], BF16)
 
         load_x_mid(0, (0, 2))
-        load_x_mid(0, (2, 4))
         load_x(0, 0)
+        load_w(0, E // 2)
+        load_x_mid(0, (2, 4))
         load_x(0, 1)
+        load_w(E // 2, E)
         load_x_mid(0, (4, 6))
-        load_w()
-        load_w()
-        load_x_mid(0, (6, H))
         nc.sync.dma_start(out=bfx_bc[:], in_=bfx.partition_broadcast(P))
+        load_x_mid(0, (6, H))
         load_x(1, 0)
 
         ident_f32 = const.tile([P, P], F32)
@@ -313,7 +317,7 @@ def tile_physicsattentionbase_pa_t_kernel(tc, x, x_mid, Wfx, bfx, Wslice, bslice
             nc.vector.reciprocal(out=inv_sum[i][:], in_=sum_exp[i][:])
 
         def scale_on_vector(i, g, t):
-            if is_head(i) and i < HEADS - 2:
+            if is_head(i) and i < HEADS - 1:
                 nc.vector.tensor_scalar_mul(out=w[i][:, g, t, :], in0=w[i][:, g, t, :], scalar1=inv_sum[i][:, g, t : t + 1])
 
         def scale_on_scalar(i):
@@ -321,7 +325,7 @@ def tile_physicsattentionbase_pa_t_kernel(tc, x, x_mid, Wfx, bfx, Wslice, bslice
                 return
             for g in range(BLOCKS):
                 for t in range(PACK):
-                    if (g, t) not in VECTOR_SCALED or i >= HEADS - 2:
+                    if (g, t) not in VECTOR_SCALED or i == HEADS - 1:
                         nc.scalar.activation(
                             out=w[i][:, g, t, :], in_=w[i][:, g, t, :], func=ACT.Copy, scale=inv_sum[i][:, g, t : t + 1]
                         )
@@ -367,14 +371,22 @@ def tile_physicsattentionbase_pa_t_kernel(tc, x, x_mid, Wfx, bfx, Wslice, bslice
             if not is_head(i):
                 return
             n_grouped[i] = work.tile([P, BLOCKS, S, PACK], BF16, name="n_grouped", tag="n_grouped", bufs=3, align_bytes=64)
+            from_end = HEADS - i
+            quarters = GPSIMD_QUARTERS_AT_END[-from_end] if from_end <= len(GPSIMD_QUARTERS_AT_END) else 4
             for g in range(BLOCKS):
-                engine = nc.vector if g == 1 and i >= HEADS - 4 else nc.gpsimd
-                engine.tensor_tensor(
-                    out=n_grouped[i][:, g].rearrange("p (c i) t -> p c t i", i=4),
-                    in0=w[i][:, g].rearrange("p t (c i) -> p c t i", i=4),
-                    in1=inv_mass_bc[i][:].rearrange("p (c i) -> p c i", i=4).unsqueeze(2).to_broadcast([P, S // 4, PACK, 4]),
-                    op=ALU.mult,
-                )
+                split = min(max(quarters - 2 * g, 0), 2) * S // 2
+                for engine, first, end in ((nc.gpsimd, 0, split), (nc.vector, split, S)):
+                    if first == end:
+                        continue
+                    engine.tensor_tensor(
+                        out=n_grouped[i][:, g, first:end, :].rearrange("p (c i) t -> p c t i", i=4),
+                        in0=w[i][:, g, :, first:end].rearrange("p t (c i) -> p c t i", i=4),
+                        in1=inv_mass_bc[i][:, first:end]
+                        .rearrange("p (c i) -> p c i", i=4)
+                        .unsqueeze(2)
+                        .to_broadcast([P, (end - first) // 4, PACK, 4]),
+                        op=ALU.mult,
+                    )
 
         def quantise_head(i, grouped, codes, scales, name):
             if not is_head(i):

@@ -38,7 +38,7 @@ X_LEAD = 6
 W_PIECES = 8
 W_REGROUP = 2
 STEPS = HEADS + POOL + 1
-VECTOR_SCALED = ((0, 3), (1, 2), (1, 3))
+VECTOR_SCALED = ((0, 3), (1, 2), (1, 3), (0, 2))
 GPSIMD_QUARTERS_AT_END = (2, 1, 1, 0)
 
 FLOPS = 2 * (B * N * C * E + B * N * H * D * S + B * H * S * D * N)
@@ -169,9 +169,13 @@ def tile_physicsattentionbase_pa_t_kernel(tc, x, x_mid, Wfx, bfx, Wslice, bslice
         def regroup_w(piece):
             part, k = divmod(piece, C_PASSES)
             w_grouped[piece] = work.tile([P, W_COLS, PACK], BF16, name="w_grouped", tag="w_grouped", bufs=4, align_bytes=64)
-            nc.vector.tensor_copy(
+            nc.gpsimd.tensor_scalar(
                 out=w_grouped[piece][:],
-                in_=w_rows[k][:, :, part * W_COLS : (part + 1) * W_COLS].rearrange("q j c -> q c j"),
+                in0=w_rows[k][:, :, part * W_COLS : (part + 1) * W_COLS].rearrange("q j c -> q c j"),
+                scalar1=1.0,
+                scalar2=0.0,
+                op0=ALU.mult,
+                op1=ALU.add,
             )
 
         def quantise_w(piece):
@@ -252,11 +256,22 @@ def tile_physicsattentionbase_pa_t_kernel(tc, x, x_mid, Wfx, bfx, Wslice, bslice
             proj_ps[i, 1] = ps_proj1.tile([P, PACK, S], F32, name="proj1", tag="proj1")
             for g in range(BLOCKS):
                 with_bias = g == 1 and bias_in_psum(i)
+                if with_bias:
+                    nc.tensor.matmul(
+                        out=proj_ps[i, g][:],
+                        lhsT=ident_bf[:],
+                        rhs=bslice_bc[:].unsqueeze(1).to_broadcast([P, PACK, S]),
+                        start=True,
+                        stop=False,
+                    )
                 for t in range(PACK):
-                    region = proj_ps[i, g][:, t, :]
-                    if with_bias:
-                        nc.tensor.matmul(out=region, lhsT=ident_bf[:], rhs=bslice_bc[:], start=True, stop=False)
-                    nc.tensor.matmul(out=region, lhsT=xm_t[i][:, g, t, :], rhs=wslice_sb[:], start=not with_bias, stop=True)
+                    nc.tensor.matmul(
+                        out=proj_ps[i, g][:, t, :],
+                        lhsT=xm_t[i][:, g, t, :],
+                        rhs=wslice_sb[:],
+                        start=not with_bias,
+                        stop=not with_bias or t == PACK - 1,
+                    )
 
         def logits(i, g):
             b, h = divmod(i, H)
@@ -297,7 +312,7 @@ def tile_physicsattentionbase_pa_t_kernel(tc, x, x_mid, Wfx, bfx, Wslice, bslice
             if not is_head(i):
                 return
             b, h = divmod(i, H)
-            sum_exp[i] = stats.tile([P, BLOCKS, PACK], F32, name="sum_exp", tag="sum_exp")
+            sum_exp[i] = stats.tile([P, BLOCKS * PACK + 1], F32, name="sum_exp", tag="sum_exp")
             for g in (1, 0):
                 from_psum = g == 1 and bias_in_psum(i)
                 for t in range(PACK):
@@ -307,18 +322,22 @@ def tile_physicsattentionbase_pa_t_kernel(tc, x, x_mid, Wfx, bfx, Wslice, bslice
                         func=ACT.Exp,
                         bias=neg_max[i, g][:, t : t + 1],
                         scale=inv_temp[:, h : h + 1] if from_psum else 1.0,
-                        accum_out=sum_exp[i][:, g, t : t + 1],
+                        accum_out=sum_exp[i][:, g * PACK + t : g * PACK + t + 1],
                     )
 
         def invert_sums(i):
             if not is_head(i):
                 return
-            inv_sum[i] = stats.tile([P, BLOCKS, PACK], F32, name="inv_sum", tag="inv_sum")
-            nc.vector.reciprocal(out=inv_sum[i][:], in_=sum_exp[i][:])
+            inv_sum[i] = stats.tile([P, BLOCKS * PACK + 1], F32, name="inv_sum", tag="inv_sum", bufs=4)
+            j = i - (INV_MASS - SCALE)
+            width = BLOCKS * PACK + (1 if is_head(j) else 0)
+            nc.vector.reciprocal(out=inv_sum[i][:, :width], in_=sum_exp[i][:, :width])
+            if is_head(j):
+                inv_mass[j] = inv_sum[i][:, BLOCKS * PACK :]
 
         def scale_on_vector(i, g, t):
             if is_head(i) and i < HEADS - 1:
-                nc.vector.tensor_scalar_mul(out=w[i][:, g, t, :], in0=w[i][:, g, t, :], scalar1=inv_sum[i][:, g, t : t + 1])
+                nc.vector.tensor_scalar_mul(out=w[i][:, g, t, :], in0=w[i][:, g, t, :], scalar1=inv_sum[i][:, g * PACK + t : g * PACK + t + 1])
 
         def scale_on_scalar(i):
             if not is_head(i):
@@ -327,7 +346,7 @@ def tile_physicsattentionbase_pa_t_kernel(tc, x, x_mid, Wfx, bfx, Wslice, bslice
                 for t in range(PACK):
                     if (g, t) not in VECTOR_SCALED or i == HEADS - 1:
                         nc.scalar.activation(
-                            out=w[i][:, g, t, :], in_=w[i][:, g, t, :], func=ACT.Copy, scale=inv_sum[i][:, g, t : t + 1]
+                            out=w[i][:, g, t, :], in_=w[i][:, g, t, :], func=ACT.Copy, scale=inv_sum[i][:, g * PACK + t : g * PACK + t + 1]
                         )
 
         def add_mass(i):
@@ -347,19 +366,22 @@ def tile_physicsattentionbase_pa_t_kernel(tc, x, x_mid, Wfx, bfx, Wslice, bslice
         def sum_mass(i):
             if not is_head(i):
                 return
-            mass[i] = stats.tile([P, 1], F32, name="mass", tag="mass")
+            k = i + INV_MASS - SCALE
+            mass[i] = sum_exp[k][:, BLOCKS * PACK :] if is_head(k) else stats.tile([P, 1], F32, name="mass", tag="mass")[:]
             unread = stats.tile([P, P], F32, tag="unread")
-            nc.scalar.activation(out=unread[:], in_=small[:, i % 2, :], func=ACT.Copy, bias=0.01 / P, accum_out=mass[i][:])
+            nc.scalar.activation(out=unread[:], in_=small[:, i % 2, :], func=ACT.Copy, bias=0.01 / P, accum_out=mass[i])
 
         def invert_mass(i):
             if not is_head(i):
                 return
-            inv_mass[i] = stats.tile([P, 1], F32, name="inv_mass", tag="inv_mass")
-            nc.vector.reciprocal(out=inv_mass[i][:], in_=mass[i][:])
+            if is_head(i + INV_MASS - SCALE):
+                return
+            inv_mass[i] = stats.tile([P, 1], F32, name="inv_mass", tag="inv_mass")[:]
+            nc.vector.reciprocal(out=inv_mass[i], in_=mass[i])
 
         def spread_inv_mass(i):
             if is_head(i):
-                nc.tensor.transpose(small[:, SPREAD, :], inv_mass[i][:].to_broadcast([P, P]), ident_f32[:])
+                nc.tensor.transpose(small[:, SPREAD, :], inv_mass[i].to_broadcast([P, P]), ident_f32[:])
 
         def copy_spread(i):
             if not is_head(i):

@@ -31,7 +31,7 @@ INV_MASS = 5
 NORMALISE = 6
 QUANTISE = 7
 FX = 6
-POOL = 8
+POOL = 9
 FIRST_X = 1
 LATER_X = FX - ROW_TILES - 1
 X_LEAD = 6
@@ -40,6 +40,8 @@ W_REGROUP = 2
 STEPS = HEADS + POOL + 1
 VECTOR_SCALED = ((0, 3), (1, 2), (1, 3), (0, 2))
 GPSIMD_QUARTERS_AT_END = (2, 1, 1, 0)
+
+NORMED, FEATURES = 0, 1
 
 FLOPS = 2 * (B * N * C * E + B * N * H * D * S + B * H * S * D * N)
 
@@ -75,13 +77,10 @@ def tile_physicsattentionbase_pa_t_kernel(tc, x, x_mid, Wfx, bfx, Wslice, bslice
         mass = {}
         inv_mass = {}
         inv_mass_bc = {}
-        n_grouped = {}
-        n_codes = {}
-        n_scales = {}
         fx_ps = {}
-        fx_grouped = {}
-        fx_codes = {}
-        fx_scales = {}
+        grouped = {}
+        codes = {}
+        scales = {}
 
         def is_head(i):
             return 0 <= i < HEADS
@@ -392,7 +391,6 @@ def tile_physicsattentionbase_pa_t_kernel(tc, x, x_mid, Wfx, bfx, Wslice, bslice
         def normalise(i):
             if not is_head(i):
                 return
-            n_grouped[i] = work.tile([P, BLOCKS, S, PACK], BF16, name="n_grouped", tag="n_grouped", bufs=3, align_bytes=64)
             from_end = HEADS - i
             quarters = GPSIMD_QUARTERS_AT_END[-from_end] if from_end <= len(GPSIMD_QUARTERS_AT_END) else 4
             for g in range(BLOCKS):
@@ -401,7 +399,7 @@ def tile_physicsattentionbase_pa_t_kernel(tc, x, x_mid, Wfx, bfx, Wslice, bslice
                     if first == end:
                         continue
                     engine.tensor_tensor(
-                        out=n_grouped[i][:, g, first:end, :].rearrange("p (c i) t -> p c t i", i=4),
+                        out=grouped[i][:, NORMED, g, first:end, :].rearrange("p (c i) t -> p c t i", i=4),
                         in0=w[i][:, g, :, first:end].rearrange("p t (c i) -> p c t i", i=4),
                         in1=inv_mass_bc[i][:, first:end]
                         .rearrange("p (c i) -> p c i", i=4)
@@ -410,15 +408,15 @@ def tile_physicsattentionbase_pa_t_kernel(tc, x, x_mid, Wfx, bfx, Wslice, bslice
                         op=ALU.mult,
                     )
 
-        def quantise_head(i, grouped, codes, scales, name):
+        def quantise_head(i):
             if not is_head(i):
                 return
-            codes[i] = work.tile([P, BLOCKS, P], U32, name=name + "_codes", tag=name + "_codes", bufs=3, align_bytes=64)
-            scales[i] = work.tile([P, BLOCKS, P], U8, name=name + "_scales", tag=name + "_scales", bufs=3, align_bytes=64)
+            codes[i] = work.tile([P, 2, BLOCKS, P], U32, name="codes", tag="codes", bufs=4, align_bytes=64)
+            scales[i] = work.tile([P, 2, BLOCKS, P], U8, name="scales", tag="scales", bufs=4, align_bytes=64)
             nc.vector.quantize_mx(
-                out=codes[i][:].rearrange("p g c -> p (g c)").bitcast(FP8X4),
-                scales=scales[i][:].rearrange("p g c -> p (g c)"),
-                in_=grouped[i][:].rearrange("p g c t -> p (g c t)"),
+                out=codes[i][:].rearrange("p n g c -> p (n g c)").bitcast(FP8X4),
+                scales=scales[i][:].rearrange("p n g c -> p (n g c)"),
+                in_=grouped[i][:].rearrange("p n g c t -> p (n g c t)"),
             )
 
         def multiply_features(i):
@@ -444,9 +442,9 @@ def tile_physicsattentionbase_pa_t_kernel(tc, x, x_mid, Wfx, bfx, Wslice, bslice
                 return
             b, h = divmod(i, H)
             if g == 0:
-                fx_grouped[i] = work.tile([P, BLOCKS, D, PACK], BF16, name="fx_grouped", tag="fx_grouped", align_bytes=64)
+                grouped[i] = work.tile([P, 2, BLOCKS, P, PACK], BF16, name="grouped", tag="grouped", bufs=3, align_bytes=64)
             nc.vector.tensor_tensor(
-                out=fx_grouped[i][:, g],
+                out=grouped[i][:, FEATURES, g],
                 in0=fx_ps[i, g][:].rearrange("p t d -> p d t"),
                 in1=bfx_bc[:, h * D : (h + 1) * D].unsqueeze(2).to_broadcast([P, D, PACK]),
                 op=ALU.add,
@@ -458,10 +456,10 @@ def tile_physicsattentionbase_pa_t_kernel(tc, x, x_mid, Wfx, bfx, Wslice, bslice
             for g in range(BLOCKS):
                 nc.tensor.matmul_mx(
                     out=small[:, POOLED, :],
-                    lhsT=n_codes[i][:, g, :].bitcast(FP8X4),
-                    lhsT_scale=n_scales[i][:, g, :],
-                    rhs=fx_codes[i][:, g, :].bitcast(FP8X4),
-                    rhs_scale=fx_scales[i][:, g, :],
+                    lhsT=codes[i][:, NORMED, g, :].bitcast(FP8X4),
+                    lhsT_scale=scales[i][:, NORMED, g, :],
+                    rhs=codes[i][:, FEATURES, g, :].bitcast(FP8X4),
+                    rhs_scale=scales[i][:, FEATURES, g, :],
                     start=(g == 0),
                     stop=(g == BLOCKS - 1),
                 )
@@ -482,13 +480,13 @@ def tile_physicsattentionbase_pa_t_kernel(tc, x, x_mid, Wfx, bfx, Wslice, bslice
             copy_x(step)
             softmax_begin(step - SOFTMAX)
             invert_sums(step - SCALE)
-            softmax_end(step - SOFTMAX)
             invert_mass(step - INV_MASS)
             multiply_features(step - FX)
             pool_points(step - POOL)
             add_mass(step - MASS)
             project(step - PROJECT)
             add_feature_bias(step - FX, 0)
+            softmax_end(step - SOFTMAX)
             add_feature_bias(step - FX, 1)
             for place in VECTOR_SCALED:
                 scale_on_vector(step - SCALE, *place)
@@ -499,8 +497,7 @@ def tile_physicsattentionbase_pa_t_kernel(tc, x, x_mid, Wfx, bfx, Wslice, bslice
             spread_inv_mass(step - INV_MASS)
             normalise(step - NORMALISE)
             quantise_x(step)
-            quantise_head(step - QUANTISE, fx_grouped, fx_codes, fx_scales, "fx")
-            quantise_head(step - QUANTISE, n_grouped, n_codes, n_scales, "n")
+            quantise_head(step - QUANTISE)
             for piece in pieces(step - 1):
                 quantise_w(piece)
             for piece in pieces(step):

from contextlib import ExitStack

import concourse.mybir as mybir
from concourse.masks import make_identity

F32 = mybir.dt.float32
BF16 = mybir.dt.bfloat16
U32 = mybir.dt.uint32
U8 = mybir.dt.uint8
FP8X4 = mybir.dt.float8_e4m3fn_x4
ALU = mybir.AluOpType
ACT = mybir.ActivationFunctionType
AXIS_X = mybir.AxisListType.X

B, N, C, H, D, S = 4, 1024, 1024, 8, 128, 128
E = H * D
P = 128
PACK = 4
K_PASS = P * PACK
C_PASSES = C // K_PASS
BLOCKS = N // K_PASS
HEADS = B * H
ROW_TILES = BLOCKS * PACK

XM_TRANSPOSE = 0
PROJECT = 1
SOFTMAX = 2
SCALE = 3
MASS = 4
INV_MASS = 5
NORMALISE = 6
QUANTISE = 7
FX = 6
POOL = 9
FIRST_X = 1
LATER_X = FX - ROW_TILES - 1
X_LEAD = 6
W_PIECES = 8
W_REGROUP = 2
STEPS = HEADS + POOL + 1
VECTOR_SCALED = ((0, 3), (1, 2), (1, 3), (0, 2))
GPSIMD_QUARTERS_AT_END = (2, 1, 1, 0)

NORMED, FEATURES = 0, 1

FLOPS = 2 * (B * N * C * E + B * N * H * D * S + B * H * S * D * N)


def tile_physicsattentionbase_pa_t_kernel(tc, x, x_mid, Wfx, bfx, Wslice, bslice, temp, out):
    nc = tc.nc
    with ExitStack() as stack:
        const = stack.enter_context(tc.tile_pool(name="const", bufs=1))
        rows = stack.enter_context(tc.tile_pool(name="rows", bufs=2))
        work = stack.enter_context(tc.tile_pool(name="work", bufs=2))
        stats = stack.enter_context(tc.tile_pool(name="stats", bufs=3))
        ps_xm = stack.enter_context(tc.psum_pool(name="ps_xm", bufs=1))
        ps_x = stack.enter_context(tc.psum_pool(name="ps_x", bufs=1))
        ps_proj0 = stack.enter_context(tc.psum_pool(name="ps_proj0", bufs=1))
        ps_proj1 = stack.enter_context(tc.psum_pool(name="ps_proj1", bufs=2))
        ps_fx = stack.enter_context(tc.psum_pool(name="ps_fx", bufs=2))
        ps_small = stack.enter_context(tc.psum_pool(name="ps_small", bufs=1))
        stack.enter_context(tc.manual_schedule())

        x_rows = {}
        xm_rows = {}
        x_banks = {}
        x_grouped = {}
        x_codes = {}
        x_scales = {}
        xm_bank = {}
        xm_t = {}
        proj_ps = {}
        w = {}
        neg_max = {}
        sum_exp = {}
        inv_sum = {}
        mass = {}
        inv_mass = {}
        inv_mass_bc = {}
        fx_ps = {}
        grouped = {}
        codes = {}
        scales = {}

        def is_head(i):
            return 0 <= i < HEADS

        def load_x(b, g):
            x_rows[b, g] = rows.tile([P, PACK, C], BF16, name="x_rows", tag="x_rows", bufs=4)
            nc.sync.dma_start(
                out=x_rows[b, g][:].rearrange("p t c -> p (t c)"),
                in_=x[b, g * K_PASS : (g + 1) * K_PASS, :].rearrange("(p t) c -> p (t c)", t=PACK),
            )

        def load_x_mid(b, heads=(0, H)):
            first, end = heads
            for g in range(BLOCKS):
                if first == 0:
                    xm_rows[b, g] = rows.tile([P, PACK, E], BF16, name="xm_rows", tag="xm_rows", bufs=4)
                nc.sync.dma_start(
                    out=xm_rows[b, g][:, :, first * D : end * D],
                    in_=x_mid[b, g * K_PASS : (g + 1) * K_PASS, first:end, :].rearrange("(p t) h d -> p t (h d)", t=PACK),
                )

        w_rows = []

        def load_w(first, end):
            for k in range(C_PASSES):
                if first == 0:
                    w_rows.append(rows.tile([P, PACK, E], BF16, name="w_rows", tag="w_rows"))
                for u in range(2):
                    start = k * K_PASS + u * 2 * P
                    nc.sync.dma_start(
                        out=w_rows[k][:, 2 * u : 2 * u + 2, first:end],
                        in_=Wfx[start : start + 2 * P, first:end].rearrange("(q e) c -> q e c", e=2),
                    )

        def load_rows(step):
            for n in range(BLOCKS + 1, B * BLOCKS):
                b, g = divmod(n, BLOCKS)
                if step == max(FIRST_X + 3, H * b + LATER_X + PACK * g - X_LEAD):
                    load_x(b, g)
            b, h = divmod(step, H)
            if h == 3 and b + 1 < B:
                load_x_mid(b + 1)

        temp_bc = const.tile([P, H], BF16)
        nc.scalar.dma_start(out=temp_bc[:], in_=temp.rearrange("a b h c -> (a b h c)").partition_broadcast(P))
        bslice_bc = const.tile([P, S], BF16)
        nc.scalar.dma_start(out=bslice_bc[:], in_=bslice.partition_broadcast(P))
        wslice_sb = const.tile([P, S], BF16)
        nc.scalar.dma_start(out=wslice_sb[:], in_=Wslice)
        bfx_bc = const.tile([P, E], BF16)

        load_x_mid(0, (0, 2))
        load_x(0, 0)
        load_w(0, E // 2)
        load_x_mid(0, (2, 4))
        load_x(0, 1)
        load_w(E // 2, E)
        load_x_mid(0, (4, 6))
        nc.sync.dma_start(out=bfx_bc[:], in_=bfx.partition_broadcast(P))
        load_x_mid(0, (6, H))
        load_x(1, 0)

        ident_f32 = const.tile([P, P], F32)
        make_identity(nc, ident_f32[:])
        ident_bf = const.tile([P, P], BF16)
        make_identity(nc, ident_bf[:])

        temp_f32 = const.tile([P, H], F32)
        nc.vector.tensor_copy(out=temp_f32[:], in_=temp_bc[:])
        inv_temp = const.tile([P, H], F32)
        nc.vector.reciprocal(out=inv_temp[:], in_=temp_f32[:])
        bias_over_temp = const.tile([P, H, S], F32)
        for h in range(H):
            nc.vector.tensor_scalar_mul(out=bias_over_temp[:, h, :], in0=bslice_bc[:], scalar1=inv_temp[:, h : h + 1])

        w_codes = const.tile([P, C_PASSES, E], U32, align_bytes=64)
        w_scales = const.tile([P, C_PASSES, E], U8, align_bytes=64)
        w_grouped = {}
        W_COLS = C_PASSES * E // W_PIECES

        def pieces(step):
            first = 2 * (step - W_REGROUP)
            return range(first, first + 2) if 0 <= first < W_PIECES else ()

        def regroup_w(piece):
            part, k = divmod(piece, C_PASSES)
            w_grouped[piece] = work.tile([P, W_COLS, PACK], BF16, name="w_grouped", tag="w_grouped", bufs=4, align_bytes=64)
            nc.gpsimd.tensor_scalar(
                out=w_grouped[piece][:],
                in0=w_rows[k][:, :, part * W_COLS : (part + 1) * W_COLS].rearrange("q j c -> q c j"),
                scalar1=1.0,
                scalar2=0.0,
                op0=ALU.mult,
                op1=ALU.add,
            )

        def quantise_w(piece):
            part, k = divmod(piece, C_PASSES)
            nc.vector.quantize_mx(
                out=w_codes[:, k, part * W_COLS : (part + 1) * W_COLS].bitcast(FP8X4),
                scales=w_scales[:, k, part * W_COLS : (part + 1) * W_COLS],
                in_=w_grouped[piece][:].rearrange("q c j -> q (c j)"),
            )

        small = ps_small.tile([P, 4, P], F32)
        SPREAD, POOLED = 2, 3

        def row_tiles(step):
            if 0 <= step - FIRST_X < ROW_TILES // 2:
                return [(0, 2 * (step - FIRST_X) + i) for i in range(2)]
            b, r = divmod(step - LATER_X, H)
            return [(b, r)] if 1 <= b < B else []

        def transpose_x(step):
            x_banks[step] = []
            for b, r in row_tiles(step):
                g, t = divmod(r, PACK)
                if b == 0:
                    bank = ps_fx.tile([P, C_PASSES, 2 * P], F32, name="first_x", tag="fx_ps")
                else:
                    bank = ps_x.tile([P, C_PASSES, 2 * P], F32, name="later_x", tag="later_x")
                x_banks[step].append((b, r, bank))
                words = x_rows[b, g][:, t, :].bitcast(F32)
                for k in range(C_PASSES):
                    for half in range(2):
                        first = (k * 2 + half) * P
                        nc.tensor.transpose(bank[:, k, half * P : (half + 1) * P], words[:, first : first + P], ident_f32[:])

        def copy_x(step):
            for b, r, bank in x_banks.get(step - 1, []):
                x_grouped[b, r] = work.tile([P, C_PASSES, P, PACK], BF16, name="x_grouped", tag="x_grouped", bufs=4, align_bytes=64)
                nc.scalar.copy(
                    out=x_grouped[b, r][:].bitcast(F32),
                    in_=bank[:].rearrange("q k (u p) -> q k p u", u=2),
                )

        def quantise_x(step):
            for b, r, bank in x_banks.get(step - 1, []):
                if r == 0:
                    x_codes[b] = work.tile([P, ROW_TILES, C_PASSES, P], U32, name="x_codes", tag="x_codes", bufs=3, align_bytes=64)
                    x_scales[b] = work.tile([P, ROW_TILES, C_PASSES, P], U8, name="x_scales", tag="x_scales", bufs=3, align_bytes=64)
                nc.vector.quantize_mx(
                    out=x_codes[b][:, r].rearrange("q k p -> q (k p)").bitcast(FP8X4),
                    scales=x_scales[b][:, r].rearrange("q k p -> q (k p)"),
                    in_=x_grouped[b, r][:].rearrange("q k p j -> q (k p j)"),
                )

        def transpose_x_mid(i):
            if not is_head(i):
                return
            b, h = divmod(i, H)
            xm_bank[i] = ps_xm.tile([P, BLOCKS, PACK, P], BF16, name="xm_bank", tag="xm_bank")
            for g in range(BLOCKS):
                for t in range(PACK):
                    nc.tensor.transpose(xm_bank[i][:, g, t, :], xm_rows[b, g][:, t, h * D : (h + 1) * D], ident_bf[:])

        def copy_x_mid(i):
            if not is_head(i):
                return
            xm_t[i] = work.tile([P, BLOCKS, PACK, P], BF16, name="xm_t", tag="xm_t")
            nc.scalar.copy(
                out=xm_t[i][:].rearrange("d g t p -> d (g t p)"), in_=xm_bank[i][:].rearrange("d g t p -> d (g t p)")
            )

        def bias_in_psum(i):
            return i < HEADS - 1

        def project(i):
            if not is_head(i):
                return
            proj_ps[i, 0] = ps_proj0.tile([P, PACK, S], F32, name="proj0", tag="proj0")
            proj_ps[i, 1] = ps_proj1.tile([P, PACK, S], F32, name="proj1", tag="proj1")
            for g in range(BLOCKS):
                with_bias = g == 1 and bias_in_psum(i)
                if with_bias:
                    nc.tensor.matmul(
                        out=proj_ps[i, g][:],
                        lhsT=ident_bf[:],
                        rhs=bslice_bc[:].unsqueeze(1).to_broadcast([P, PACK, S]),
                        start=True,
                        stop=False,
                    )
                for t in range(PACK):
                    nc.tensor.matmul(
                        out=proj_ps[i, g][:, t, :],
                        lhsT=xm_t[i][:, g, t, :],
                        rhs=wslice_sb[:],
                        start=not with_bias,
                        stop=not with_bias or t == PACK - 1,
                    )

        def logits(i, g):
            b, h = divmod(i, H)
            nc.vector.scalar_tensor_tensor(
                out=w[i][:, g],
                in0=proj_ps[i, g][:],
                scalar=inv_temp[:, h : h + 1],
                in1=bias_over_temp[:, h, :].unsqueeze(1).to_broadcast([P, PACK, S]),
                op0=ALU.mult,
                op1=ALU.add,
            )

        def row_max(i, g, source):
            nc.vector.tensor_reduce(out=neg_max[i, g][:], in_=source, axis=AXIS_X, op=ALU.max, negate=True)

        def softmax_begin(i):
            if not is_head(i):
                return
            b, h = divmod(i, H)
            w[i] = work.tile([P, BLOCKS, PACK, S], F32, name="w", tag="w", bufs=7)
            for g in range(BLOCKS):
                neg_max[i, g] = stats.tile([P, PACK], F32, name="neg_max", tag="neg_max%d" % g)
            if bias_in_psum(i):
                raw = stats.tile([P, PACK], F32, tag="raw_max")
                nc.vector.tensor_reduce(out=raw[:], in_=proj_ps[i, 1][:], axis=AXIS_X, op=ALU.max, negate=True)
                logits(i, 0)
                nc.vector.tensor_scalar_mul(out=neg_max[i, 1][:], in0=raw[:], scalar1=inv_temp[:, h : h + 1])
            else:
                logits(i, 1)
                logits(i, 0)
                row_max(i, 1, w[i][:, 1])

        def softmax_end(i):
            if is_head(i):
                row_max(i, 0, w[i][:, 0])

        def exponentials(i):
            if not is_head(i):
                return
            b, h = divmod(i, H)
            sum_exp[i] = stats.tile([P, BLOCKS * PACK + 1], F32, name="sum_exp", tag="sum_exp")
            for g in (1, 0):
                from_psum = g == 1 and bias_in_psum(i)
                for t in range(PACK):
                    nc.scalar.activation(
                        out=w[i][:, g, t, :],
                        in_=proj_ps[i, g][:, t, :] if from_psum else w[i][:, g, t, :],
                        func=ACT.Exp,
                        bias=neg_max[i, g][:, t : t + 1],
                        scale=inv_temp[:, h : h + 1] if from_psum else 1.0,
                        accum_out=sum_exp[i][:, g * PACK + t : g * PACK + t + 1],
                    )

        def invert_sums(i):
            if not is_head(i):
                return
            inv_sum[i] = stats.tile([P, BLOCKS * PACK + 1], F32, name="inv_sum", tag="inv_sum", bufs=4)
            j = i - (INV_MASS - SCALE)
            width = BLOCKS * PACK + (1 if is_head(j) else 0)
            nc.vector.reciprocal(out=inv_sum[i][:, :width], in_=sum_exp[i][:, :width])
            if is_head(j):
                inv_mass[j] = inv_sum[i][:, BLOCKS * PACK :]

        def scale_on_vector(i, g, t):
            if is_head(i) and i < HEADS - 1:
                nc.vector.tensor_scalar_mul(out=w[i][:, g, t, :], in0=w[i][:, g, t, :], scalar1=inv_sum[i][:, g * PACK + t : g * PACK + t + 1])

        def scale_on_scalar(i):
            if not is_head(i):
                return
            for g in range(BLOCKS):
                for t in range(PACK):
                    if (g, t) not in VECTOR_SCALED or i == HEADS - 1:
                        nc.scalar.activation(
                            out=w[i][:, g, t, :], in_=w[i][:, g, t, :], func=ACT.Copy, scale=inv_sum[i][:, g * PACK + t : g * PACK + t + 1]
                        )

        def add_mass(i):
            if not is_head(i):
                return
            for g in range(BLOCKS):
                for t in range(PACK):
                    nc.tensor.matmul(
                        out=small[:, i % 2, :],
                        lhsT=w[i][:, g, t, :],
                        rhs=ident_f32[:],
                        is_transpose=True,
                        start=(g == 0 and t == 0),
                        stop=(g == BLOCKS - 1 and t == PACK - 1),
                    )

        def sum_mass(i):
            if not is_head(i):
                return
            k = i + INV_MASS - SCALE
            mass[i] = sum_exp[k][:, BLOCKS * PACK :] if is_head(k) else stats.tile([P, 1], F32, name="mass", tag="mass")[:]
            unread = stats.tile([P, P], F32, tag="unread")
            nc.scalar.activation(out=unread[:], in_=small[:, i % 2, :], func=ACT.Copy, bias=0.01 / P, accum_out=mass[i])

        def invert_mass(i):
            if not is_head(i):
                return
            if is_head(i + INV_MASS - SCALE):
                return
            inv_mass[i] = stats.tile([P, 1], F32, name="inv_mass", tag="inv_mass")[:]
            nc.vector.reciprocal(out=inv_mass[i], in_=mass[i])

        def spread_inv_mass(i):
            if is_head(i):
                nc.tensor.transpose(small[:, SPREAD, :], inv_mass[i].to_broadcast([P, P]), ident_f32[:])

        def copy_spread(i):
            if not is_head(i):
                return
            inv_mass_bc[i] = stats.tile([P, S], F32, name="inv_mass_bc", tag="inv_mass_bc")
            nc.scalar.copy(out=inv_mass_bc[i][:], in_=small[:, SPREAD, :])

        def normalise(i):
            if not is_head(i):
                return
            from_end = HEADS - i
            quarters = GPSIMD_QUARTERS_AT_END[-from_end] if from_end <= len(GPSIMD_QUARTERS_AT_END) else 4
            for g in range(BLOCKS):
                split = min(max(quarters - 2 * g, 0), 2) * S // 2
                for engine, first, end in ((nc.gpsimd, 0, split), (nc.vector, split, S)):
                    if first == end:
                        continue
                    engine.tensor_tensor(
                        out=grouped[i][:, NORMED, g, first:end, :].rearrange("p (c i) t -> p c t i", i=4),
                        in0=w[i][:, g, :, first:end].rearrange("p t (c i) -> p c t i", i=4),
                        in1=inv_mass_bc[i][:, first:end]
                        .rearrange("p (c i) -> p c i", i=4)
                        .unsqueeze(2)
                        .to_broadcast([P, (end - first) // 4, PACK, 4]),
                        op=ALU.mult,
                    )

        def quantise_head(i):
            if not is_head(i):
                return
            codes[i] = work.tile([P, 2, BLOCKS, P], U32, name="codes", tag="codes", bufs=4, align_bytes=64)
            scales[i] = work.tile([P, 2, BLOCKS, P], U8, name="scales", tag="scales", bufs=4, align_bytes=64)
            nc.vector.quantize_mx(
                out=codes[i][:].rearrange("p n g c -> p (n g c)").bitcast(FP8X4),
                scales=scales[i][:].rearrange("p n g c -> p (n g c)"),
                in_=grouped[i][:].rearrange("p n g c t -> p (n g c t)"),
            )

        def multiply_features(i):
            if not is_head(i):
                return
            b, h = divmod(i, H)
            for g in range(BLOCKS):
                fx_ps[i, g] = ps_fx.tile([P, PACK, D], F32, name="fx_ps", tag="fx_ps")
                for t in range(PACK):
                    for k in range(C_PASSES):
                        nc.tensor.matmul_mx(
                            out=fx_ps[i, g][:, t, :],
                            lhsT=x_codes[b][:, g * PACK + t, k, :].bitcast(FP8X4),
                            lhsT_scale=x_scales[b][:, g * PACK + t, k, :],
                            rhs=w_codes[:, k, h * D : (h + 1) * D].bitcast(FP8X4),
                            rhs_scale=w_scales[:, k, h * D : (h + 1) * D],
                            start=(k == 0),
                            stop=(k == C_PASSES - 1),
                        )

        def add_feature_bias(i, g):
            if not is_head(i):
                return
            b, h = divmod(i, H)
            if g == 0:
                grouped[i] = work.tile([P, 2, BLOCKS, P, PACK], BF16, name="grouped", tag="grouped", bufs=3, align_bytes=64)
            nc.vector.tensor_tensor(
                out=grouped[i][:, FEATURES, g],
                in0=fx_ps[i, g][:].rearrange("p t d -> p d t"),
                in1=bfx_bc[:, h * D : (h + 1) * D].unsqueeze(2).to_broadcast([P, D, PACK]),
                op=ALU.add,
            )

        def pool_points(i):
            if not is_head(i):
                return
            for g in range(BLOCKS):
                nc.tensor.matmul_mx(
                    out=small[:, POOLED, :],
                    lhsT=codes[i][:, NORMED, g, :].bitcast(FP8X4),
                    lhsT_scale=scales[i][:, NORMED, g, :],
                    rhs=codes[i][:, FEATURES, g, :].bitcast(FP8X4),
                    rhs_scale=scales[i][:, FEATURES, g, :],
                    start=(g == 0),
                    stop=(g == BLOCKS - 1),
                )

        def copy_out(i):
            if not is_head(i):
                return
            out_sb = work.tile([P, D], F32, tag="out_sb", bufs=4)
            nc.scalar.copy(out=out_sb[:], in_=small[:, POOLED, :])
            nc.sync.dma_start(out=out[i // H, i % H], in_=out_sb[:])

        for step in range(STEPS):
            load_rows(step)
            copy_spread(step - NORMALISE)
            sum_mass(step - INV_MASS)
            copy_out(step - POOL - 1)
            copy_x_mid(step - PROJECT)
            copy_x(step)
            softmax_begin(step - SOFTMAX)
            invert_sums(step - SCALE)
            invert_mass(step - INV_MASS)
            multiply_features(step - FX)
            pool_points(step - POOL)
            add_mass(step - MASS)
            project(step - PROJECT)
            add_feature_bias(step - FX, 0)
            softmax_end(step - SOFTMAX)
            add_feature_bias(step - FX, 1)
            for place in VECTOR_SCALED:
                scale_on_vector(step - SCALE, *place)
            scale_on_scalar(step - SCALE)
            exponentials(step - SOFTMAX)
            transpose_x_mid(step)
            transpose_x(step)
            spread_inv_mass(step - INV_MASS)
            normalise(step - NORMALISE)
            quantise_x(step)
            quantise_head(step - QUANTISE)
            for piece in pieces(step - 1):
                quantise_w(piece)
            for piece in pieces(step):
                regroup_w(piece)
